import numpy as np
import ml_dtypes

BF16 = ml_dtypes.bfloat16


def bf(x):
    return np.asarray(x, np.float32).astype(BF16)


def f32(x):
    return np.asarray(x, np.float32)


def f64(x):
    return np.asarray(x).astype(np.float64)


def striped(idx):
    return np.tile(idx.reshape(-1, 16).T, (8, 1))


C, E, S, NLOC, NNEI, H, K, N = 1024, 128, 2048, 128, 32, 1024, 4, 4096
RES = np.sqrt(5.0)
WSCALE = 3.0


def setup_inputs():
    return {"x": f32(np.random.standard_normal((C, S))), "edge": bf(np.random.standard_normal((E, N))), "w_proj": bf(WSCALE * np.random.standard_normal((E, C)) / np.sqrt(E)), "sw": f32(np.random.uniform(0.0, 1.0, (1, N))), "offs": striped(np.concatenate([np.random.permutation(S)[:H] for _ in range(K)]))}


def reference(x, edge, w_proj, sw, offs):
    idx = offs[:16].T.reshape(-1)
    p = (f64(w_proj).T @ f64(edge)) * f64(sw)
    msg = f64(x)[:, idx] * p
    conv = msg.reshape(C, NLOC, NNEI).sum(axis=2) / NNEI
    return (f64(x)[:, :NLOC] + conv) / RES

@@ -1,0 +1,70 @@
+import math
+
+import concourse.mybir as mybir
+
+F32 = mybir.dt.float32
+BF16 = mybir.dt.bfloat16
+U16 = mybir.dt.uint16
+MULT = mybir.AluOpType.mult
+ADD = mybir.AluOpType.add
+
+P = 128
+C, S = 1024, 2048
+E, N = 128, 4096
+NLOC, NNEI = 128, 32
+BANK = 512
+PIECE = 1024
+
+FLOPS = 2 * C * E * N
+
+
+def tile_repflowlayer_kernel(tc, x, edge, w_proj, sw, offs, out):
+    nc = tc.nc
+    x_blocks = x.rearrange("(b p) s -> b p s", p=P)
+    out_blocks = out.rearrange("(b p) i -> b p i", p=P)
+    sw_row = sw.rearrange("o n -> (o n)")
+
+    with (
+        tc.tile_pool(name="held", bufs=1) as held,
+        tc.tile_pool(name="tables", bufs=2) as tables,
+        tc.tile_pool(name="work", bufs=2) as work,
+        tc.psum_pool(name="psum", bufs=4) as psum,
+    ):
+        offsets = held.tile([P, N // 16], U16, name="offsets")
+        nc.sync.dma_start(offsets[:], offs)
+        edge_sb = held.tile([E, N], BF16, name="edge_sb")
+        nc.scalar.dma_start(edge_sb[:], edge)
+        w_sb = held.tile([E, C], BF16, name="w_sb")
+        nc.scalar.dma_start(w_sb[:], w_proj)
+        sw_all = held.tile([P, N], F32, name="sw_all")
+        nc.gpsimd.dma_start(sw_all[:], sw_row.partition_broadcast(P))
+
+        for b in range(C // P):
+            x_blk = tables.tile([P, S], F32, name="x_blk")
+            nc.sync.dma_start(x_blk[:], x_blocks[b])
+            conv = work.tile([P, NLOC], F32, name="conv")
+            for k in range(N // PIECE):
+                p_sb = work.tile([P, PIECE], F32, name="p_sb")
+                for h in range(PIECE // BANK):
+                    j0 = k * PIECE + h * BANK
+                    proj = psum.tile([P, BANK], F32, name="proj")
+                    nc.tensor.matmul(
+                        proj[:], w_sb[:, b * P : (b + 1) * P], edge_sb[:, j0 : j0 + BANK], start=True, stop=True
+                    )
+                    nc.vector.tensor_tensor(
+                        p_sb[:, h * BANK : (h + 1) * BANK], proj[:], sw_all[:, j0 : j0 + BANK], MULT
+                    )
+                msg = work.tile([P, PIECE], F32, name="msg")
+                picked = x_blk[:].indirect(offsets[:, k * (PIECE // 16) : (k + 1) * (PIECE // 16)])
+                nc.vector.tensor_tensor(msg[:], picked, p_sb[:], MULT)
+                atoms = PIECE // NNEI
+                nc.vector.tensor_reduce(
+                    conv[:, k * atoms : (k + 1) * atoms],
+                    msg[:].rearrange("p (i t) -> p i t", t=NNEI),
+                    axis=mybir.AxisListType.X,
+                    op=ADD,
+                )
+            res = work.tile([P, NLOC], F32, name="res")
+            nc.vector.scalar_tensor_tensor(res[:], conv[:], 1.0 / NNEI, x_blk[:, 0:NLOC], MULT, ADD)
+            nc.scalar.mul(res[:], res[:], 1.0 / math.sqrt(5.0))
+            nc.sync.dma_start(out_blocks[b], res[:])

@@ -13,9 +13,9 @@ C, S = 1024, 2048
 E, N = 128, 4096
 NLOC, NNEI = 128, 32
 BANK = 512
-PIECE = 1024
 
 FLOPS = 2 * C * E * N
+PIECE = 1024
 
 
 def tile_repflowlayer_kernel(tc, x, edge, w_proj, sw, offs, out):
@@ -26,45 +26,54 @@ def tile_repflowlayer_kernel(tc, x, edge, w_proj, sw, offs, out):
 
     with (
         tc.tile_pool(name="held", bufs=1) as held,
-        tc.tile_pool(name="tables", bufs=2) as tables,
         tc.tile_pool(name="work", bufs=2) as work,
-        tc.psum_pool(name="psum", bufs=4) as psum,
+        tc.tile_pool(name="pieces", bufs=3) as pieces,
+        tc.psum_pool(name="psum", bufs=6) as psum,
     ):
         offsets = held.tile([P, N // 16], U16, name="offsets")
         nc.sync.dma_start(offsets[:], offs)
-        edge_sb = held.tile([E, N], BF16, name="edge_sb")
-        nc.scalar.dma_start(edge_sb[:], edge)
+
         w_sb = held.tile([E, C], BF16, name="w_sb")
-        nc.scalar.dma_start(w_sb[:], w_proj)
-        sw_all = held.tile([P, N], F32, name="sw_all")
-        nc.gpsimd.dma_start(sw_all[:], sw_row.partition_broadcast(P))
+        nc.sync.dma_start(w_sb[:], w_proj)
+        w_f32 = held.tile([E, C], F32, name="w_f32")
+        nc.scalar.mul(w_f32[:], w_sb[:], 1.0 / (NNEI * math.sqrt(5.0)))
+
+        x_tiles = [held.tile([P, S], F32, name=f"x{b}") for b in range(C // P)]
+        for b in range(C // P):
+            nc.scalar.dma_start(x_tiles[b][:], x_blocks[b])
+
+        edge_sb = held.tile([E, N], BF16, name="edge_sb")
+        sw_all = held.tile([E, N], F32, name="sw_all")
+        edge_sw = held.tile([E, N], F32, name="edge_sw")
+        for q in range(N // BANK):
+            cols = slice(q * BANK, (q + 1) * BANK)
+            nc.sync.dma_start(edge_sb[:, cols], edge[:, cols])
+            nc.sync.dma_start(sw_all[:, cols], sw_row[cols].partition_broadcast(E))
+            nc.gpsimd.tensor_tensor(edge_sw[:, cols], edge_sb[:, cols], sw_all[:, cols], MULT)
 
         for b in range(C // P):
-            x_blk = tables.tile([P, S], F32, name="x_blk")
-            nc.sync.dma_start(x_blk[:], x_blocks[b])
-            conv = work.tile([P, NLOC], F32, name="conv")
+            x_blk = x_tiles[b]
+            msg = work.tile([P, N], F32, name="msg")
             for k in range(N // PIECE):
-                p_sb = work.tile([P, PIECE], F32, name="p_sb")
+                p_sb = pieces.tile([P, PIECE], F32, name="p_sb")
                 for h in range(PIECE // BANK):
                     j0 = k * PIECE + h * BANK
-                    proj = psum.tile([P, BANK], F32, name="proj")
+                    p_ps = psum.tile([P, BANK], F32, name="p_ps")
                     nc.tensor.matmul(
-                        proj[:], w_sb[:, b * P : (b + 1) * P], edge_sb[:, j0 : j0 + BANK], start=True, stop=True
+                        p_ps[:], w_f32[:, b * P : (b + 1) * P], edge_sw[:, j0 : j0 + BANK], start=True, stop=True
                     )
-                    nc.vector.tensor_tensor(
-                        p_sb[:, h * BANK : (h + 1) * BANK], proj[:], sw_all[:, j0 : j0 + BANK], MULT
-                    )
-                msg = work.tile([P, PIECE], F32, name="msg")
+                    nc.scalar.copy(p_sb[:, h * BANK : (h + 1) * BANK], p_ps[:])
                 picked = x_blk[:].indirect(offsets[:, k * (PIECE // 16) : (k + 1) * (PIECE // 16)])
-                nc.vector.tensor_tensor(msg[:], picked, p_sb[:], MULT)
-                atoms = PIECE // NNEI
-                nc.vector.tensor_reduce(
-                    conv[:, k * atoms : (k + 1) * atoms],
-                    msg[:].rearrange("p (i t) -> p i t", t=NNEI),
-                    axis=mybir.AxisListType.X,
-                    op=ADD,
-                )
+                nc.vector.tensor_tensor(msg[:, k * PIECE : (k + 1) * PIECE], picked, p_sb[:], MULT)
+
+            sums = msg[:].rearrange("p (i t) -> p i t", t=NNEI)
+            for width in (16, 8, 4, 2, 1):
+                half = work.tile([P, NLOC * width], F32, name=f"half{width}")
+                halved = half[:].rearrange("p (i t) -> p i t", t=width)
+                nc.gpsimd.tensor_tensor(halved, sums[:, :, 0:width], sums[:, :, width : 2 * width], ADD)
+                sums = halved
+            own = work.tile([P, NLOC], F32, name="own")
+            nc.scalar.mul(own[:], x_blk[:, 0:NLOC], 1.0 / math.sqrt(5.0))
             res = work.tile([P, NLOC], F32, name="res")
-            nc.vector.scalar_tensor_tensor(res[:], conv[:], 1.0 / NNEI, x_blk[:, 0:NLOC], MULT, ADD)
-            nc.scalar.mul(res[:], res[:], 1.0 / math.sqrt(5.0))
+            nc.gpsimd.tensor_tensor(res[:], half[:], own[:], ADD)
             nc.sync.dma_start(out_blocks[b], res[:])

@@ -66,14 +66,10 @@ def tile_repflowlayer_kernel(tc, x, edge, w_proj, sw, offs, out):
                 picked = x_blk[:].indirect(offsets[:, k * (PIECE // 16) : (k + 1) * (PIECE // 16)])
                 nc.vector.tensor_tensor(msg[:, k * PIECE : (k + 1) * PIECE], picked, p_sb[:], MULT)
 
-            sums = msg[:].rearrange("p (i t) -> p i t", t=NNEI)
-            for width in (16, 8, 4, 2, 1):
-                half = work.tile([P, NLOC * width], F32, name=f"half{width}")
-                halved = half[:].rearrange("p (i t) -> p i t", t=width)
-                nc.gpsimd.tensor_tensor(halved, sums[:, :, 0:width], sums[:, :, width : 2 * width], ADD)
-                sums = halved
-            own = work.tile([P, NLOC], F32, name="own")
-            nc.scalar.mul(own[:], x_blk[:, 0:NLOC], 1.0 / math.sqrt(5.0))
+            conv = work.tile([P, NLOC], F32, name="conv")
+            nc.vector.tensor_reduce(
+                conv[:], msg[:].rearrange("p (i t) -> p i t", t=NNEI), axis=mybir.AxisListType.X, op=ADD
+            )
             res = work.tile([P, NLOC], F32, name="res")
-            nc.gpsimd.tensor_tensor(res[:], half[:], own[:], ADD)
+            nc.vector.scalar_tensor_tensor(res[:], x_blk[:, 0:NLOC], 1.0 / math.sqrt(5.0), conv[:], MULT, ADD)
             nc.sync.dma_start(out_blocks[b], res[:])

@@ -27,49 +27,50 @@ def tile_repflowlayer_kernel(tc, x, edge, w_proj, sw, offs, out):
     with (
         tc.tile_pool(name="held", bufs=1) as held,
         tc.tile_pool(name="work", bufs=2) as work,
-        tc.tile_pool(name="pieces", bufs=3) as pieces,
-        tc.psum_pool(name="psum", bufs=6) as psum,
+        tc.tile_pool(name="pieces", bufs=4) as pieces,
+        tc.psum_pool(name="psum", bufs=8) as psum,
     ):
         offsets = held.tile([P, N // 16], U16, name="offsets")
-        nc.sync.dma_start(offsets[:], offs)
-
         w_sb = held.tile([E, C], BF16, name="w_sb")
-        nc.sync.dma_start(w_sb[:], w_proj)
-        w_f32 = held.tile([E, C], F32, name="w_f32")
-        nc.scalar.mul(w_f32[:], w_sb[:], 1.0 / (NNEI * math.sqrt(5.0)))
-
-        x_tiles = [held.tile([P, S], F32, name=f"x{b}") for b in range(C // P)]
-        for b in range(C // P):
-            nc.scalar.dma_start(x_tiles[b][:], x_blocks[b])
-
         edge_sb = held.tile([E, N], BF16, name="edge_sb")
         sw_all = held.tile([E, N], F32, name="sw_all")
         edge_sw = held.tile([E, N], F32, name="edge_sw")
+        x_tiles = [held.tile([P, S], F32, name=f"x{b}") for b in range(C // P)]
+
+        nc.sync.dma_start(offsets[:], offs)
+        nc.sync.dma_start(w_sb[:], w_proj)
         for q in range(N // BANK):
+            if q == PIECE // BANK:
+                nc.sync.dma_start(x_tiles[0][:], x_blocks[0])
             cols = slice(q * BANK, (q + 1) * BANK)
             nc.sync.dma_start(edge_sb[:, cols], edge[:, cols])
             nc.sync.dma_start(sw_all[:, cols], sw_row[cols].partition_broadcast(E))
-            nc.gpsimd.tensor_tensor(edge_sw[:, cols], edge_sb[:, cols], sw_all[:, cols], MULT)
+            nc.vector.tensor_tensor(edge_sw[:, cols], edge_sb[:, cols], sw_all[:, cols], MULT)
+        for b in range(1, C // P):
+            nc.sync.dma_start(x_tiles[b][:], x_blocks[b])
 
         for b in range(C // P):
             x_blk = x_tiles[b]
-            msg = work.tile([P, N], F32, name="msg")
+            w_blk = work.tile([E, P], F32, name="w_blk")
+            nc.scalar.mul(w_blk[:], w_sb[:, b * P : (b + 1) * P], 1.0 / (NNEI * math.sqrt(5.0)))
+            conv = work.tile([P, NLOC], F32, name="conv")
             for k in range(N // PIECE):
                 p_sb = pieces.tile([P, PIECE], F32, name="p_sb")
                 for h in range(PIECE // BANK):
                     j0 = k * PIECE + h * BANK
                     p_ps = psum.tile([P, BANK], F32, name="p_ps")
-                    nc.tensor.matmul(
-                        p_ps[:], w_f32[:, b * P : (b + 1) * P], edge_sw[:, j0 : j0 + BANK], start=True, stop=True
-                    )
+                    nc.tensor.matmul(p_ps[:], w_blk[:], edge_sw[:, j0 : j0 + BANK], start=True, stop=True)
                     nc.scalar.copy(p_sb[:, h * BANK : (h + 1) * BANK], p_ps[:])
+                msg = pieces.tile([P, PIECE], F32, name="msg")
                 picked = x_blk[:].indirect(offsets[:, k * (PIECE // 16) : (k + 1) * (PIECE // 16)])
-                nc.vector.tensor_tensor(msg[:, k * PIECE : (k + 1) * PIECE], picked, p_sb[:], MULT)
-
-            conv = work.tile([P, NLOC], F32, name="conv")
-            nc.vector.tensor_reduce(
-                conv[:], msg[:].rearrange("p (i t) -> p i t", t=NNEI), axis=mybir.AxisListType.X, op=ADD
-            )
+                nc.vector.tensor_tensor(msg[:], picked, p_sb[:], MULT)
+                atoms = PIECE // NNEI
+                nc.vector.tensor_reduce(
+                    conv[:, k * atoms : (k + 1) * atoms],
+                    msg[:].rearrange("p (i t) -> p i t", t=NNEI),
+                    axis=mybir.AxisListType.X,
+                    op=ADD,
+                )
             res = work.tile([P, NLOC], F32, name="res")
             nc.vector.scalar_tensor_tensor(res[:], x_blk[:, 0:NLOC], 1.0 / math.sqrt(5.0), conv[:], MULT, ADD)
             nc.sync.dma_start(out_blocks[b], res[:])

@@ -7,6 +7,7 @@ BF16 = mybir.dt.bfloat16
 U16 = mybir.dt.uint16
 MULT = mybir.AluOpType.mult
 ADD = mybir.AluOpType.add
+COPY = mybir.ActivationFunctionType.Copy
 
 P = 128
 C, S = 1024, 2048
@@ -36,15 +37,16 @@ def tile_repflowlayer_kernel(tc, x, edge, w_proj, sw, offs, out):
         sw_all = held.tile([E, N], F32, name="sw_all")
         edge_sw = held.tile([E, N], F32, name="edge_sw")
         x_tiles = [held.tile([P, S], F32, name=f"x{b}") for b in range(C // P)]
+        unread = held.tile([P, NNEI], F32, name="unread")
 
         nc.sync.dma_start(offsets[:], offs)
-        nc.sync.dma_start(w_sb[:], w_proj)
-        for q in range(N // BANK):
-            if q == PIECE // BANK:
-                nc.sync.dma_start(x_tiles[0][:], x_blocks[0])
-            cols = slice(q * BANK, (q + 1) * BANK)
-            nc.sync.dma_start(edge_sb[:, cols], edge[:, cols])
+        nc.scalar.dma_start(w_sb[:], w_proj)
+        for k in range(N // PIECE):
+            cols = slice(k * PIECE, (k + 1) * PIECE)
             nc.sync.dma_start(sw_all[:, cols], sw_row[cols].partition_broadcast(E))
+            nc.scalar.dma_start(edge_sb[:, cols], edge[:, cols])
+            if k == 0:
+                nc.scalar.dma_start(x_tiles[0][:], x_blocks[0])
             nc.vector.tensor_tensor(edge_sw[:, cols], edge_sb[:, cols], sw_all[:, cols], MULT)
         for b in range(1, C // P):
             nc.sync.dma_start(x_tiles[b][:], x_blocks[b])
@@ -65,12 +67,21 @@ def tile_repflowlayer_kernel(tc, x, edge, w_proj, sw, offs, out):
                 picked = x_blk[:].indirect(offsets[:, k * (PIECE // 16) : (k + 1) * (PIECE // 16)])
                 nc.vector.tensor_tensor(msg[:], picked, p_sb[:], MULT)
                 atoms = PIECE // NNEI
-                nc.vector.tensor_reduce(
-                    conv[:, k * atoms : (k + 1) * atoms],
-                    msg[:].rearrange("p (i t) -> p i t", t=NNEI),
-                    axis=mybir.AxisListType.X,
-                    op=ADD,
-                )
+                if (b * (N // PIECE) + k) % 3 == 2:
+                    for i in range(atoms):
+                        nc.scalar.activation(
+                            unread[:],
+                            msg[:, i * NNEI : (i + 1) * NNEI],
+                            COPY,
+                            accum_out=conv[:, k * atoms + i : k * atoms + i + 1],
+                        )
+                else:
+                    nc.vector.tensor_reduce(
+                        conv[:, k * atoms : (k + 1) * atoms],
+                        msg[:].rearrange("p (i t) -> p i t", t=NNEI),
+                        axis=mybir.AxisListType.X,
+                        op=ADD,
+                    )
             res = work.tile([P, NLOC], F32, name="res")
             nc.vector.scalar_tensor_tensor(res[:], x_blk[:, 0:NLOC], 1.0 / math.sqrt(5.0), conv[:], MULT, ADD)
             nc.sync.dma_start(out_blocks[b], res[:])

@@ -7,16 +7,16 @@ BF16 = mybir.dt.bfloat16
 U16 = mybir.dt.uint16
 MULT = mybir.AluOpType.mult
 ADD = mybir.AluOpType.add
-COPY = mybir.ActivationFunctionType.Copy
 
 P = 128
 C, S = 1024, 2048
 E, N = 128, 4096
 NLOC, NNEI = 128, 32
 BANK = 512
+PIECE = 1024
+ATOMS = PIECE // NNEI
 
 FLOPS = 2 * C * E * N
-PIECE = 1024
 
 
 def tile_repflowlayer_kernel(tc, x, edge, w_proj, sw, offs, out):
@@ -27,8 +27,8 @@ def tile_repflowlayer_kernel(tc, x, edge, w_proj, sw, offs, out):
 
     with (
         tc.tile_pool(name="held", bufs=1) as held,
-        tc.tile_pool(name="work", bufs=2) as work,
-        tc.tile_pool(name="pieces", bufs=4) as pieces,
+        tc.tile_pool(name="per_block", bufs=2) as per_block,
+        tc.tile_pool(name="per_piece", bufs=4) as per_piece,
         tc.psum_pool(name="psum", bufs=8) as psum,
     ):
         offsets = held.tile([P, N // 16], U16, name="offsets")
@@ -37,7 +37,6 @@ def tile_repflowlayer_kernel(tc, x, edge, w_proj, sw, offs, out):
         sw_all = held.tile([E, N], F32, name="sw_all")
         edge_sw = held.tile([E, N], F32, name="edge_sw")
         x_tiles = [held.tile([P, S], F32, name=f"x{b}") for b in range(C // P)]
-        unread = held.tile([P, NNEI], F32, name="unread")
 
         nc.sync.dma_start(offsets[:], offs)
         nc.scalar.dma_start(w_sb[:], w_proj)
@@ -53,35 +52,25 @@ def tile_repflowlayer_kernel(tc, x, edge, w_proj, sw, offs, out):
 
         for b in range(C // P):
             x_blk = x_tiles[b]
-            w_blk = work.tile([E, P], F32, name="w_blk")
+            w_blk = per_block.tile([E, P], F32, name="w_blk")
             nc.scalar.mul(w_blk[:], w_sb[:, b * P : (b + 1) * P], 1.0 / (NNEI * math.sqrt(5.0)))
-            conv = work.tile([P, NLOC], F32, name="conv")
+            conv = per_block.tile([P, NLOC], F32, name="conv")
             for k in range(N // PIECE):
-                p_sb = pieces.tile([P, PIECE], F32, name="p_sb")
+                p_sb = per_piece.tile([P, PIECE], F32, name="p_sb")
                 for h in range(PIECE // BANK):
                     j0 = k * PIECE + h * BANK
                     p_ps = psum.tile([P, BANK], F32, name="p_ps")
                     nc.tensor.matmul(p_ps[:], w_blk[:], edge_sw[:, j0 : j0 + BANK], start=True, stop=True)
                     nc.scalar.copy(p_sb[:, h * BANK : (h + 1) * BANK], p_ps[:])
-                msg = pieces.tile([P, PIECE], F32, name="msg")
+                msg = per_piece.tile([P, PIECE], F32, name="msg")
                 picked = x_blk[:].indirect(offsets[:, k * (PIECE // 16) : (k + 1) * (PIECE // 16)])
                 nc.vector.tensor_tensor(msg[:], picked, p_sb[:], MULT)
-                atoms = PIECE // NNEI
-                if (b * (N // PIECE) + k) % 3 == 2:
-                    for i in range(atoms):
-                        nc.scalar.activation(
-                            unread[:],
-                            msg[:, i * NNEI : (i + 1) * NNEI],
-                            COPY,
-                            accum_out=conv[:, k * atoms + i : k * atoms + i + 1],
-                        )
-                else:
-                    nc.vector.tensor_reduce(
-                        conv[:, k * atoms : (k + 1) * atoms],
-                        msg[:].rearrange("p (i t) -> p i t", t=NNEI),
-                        axis=mybir.AxisListType.X,
-                        op=ADD,
-                    )
-            res = work.tile([P, NLOC], F32, name="res")
+                nc.vector.tensor_reduce(
+                    conv[:, k * ATOMS : (k + 1) * ATOMS],
+                    msg[:].rearrange("p (i t) -> p i t", t=NNEI),
+                    axis=mybir.AxisListType.X,
+                    op=ADD,
+                )
+            res = per_block.tile([P, NLOC], F32, name="res")
             nc.vector.scalar_tensor_tensor(res[:], x_blk[:, 0:NLOC], 1.0 / math.sqrt(5.0), conv[:], MULT, ADD)
             nc.sync.dma_start(out_blocks[b], res[:])

@@ -44,10 +44,8 @@ def tile_repflowlayer_kernel(tc, x, edge, w_proj, sw, offs, out):
             cols = slice(k * PIECE, (k + 1) * PIECE)
             nc.sync.dma_start(sw_all[:, cols], sw_row[cols].partition_broadcast(E))
             nc.scalar.dma_start(edge_sb[:, cols], edge[:, cols])
-            if k == 0:
-                nc.scalar.dma_start(x_tiles[0][:], x_blocks[0])
             nc.vector.tensor_tensor(edge_sw[:, cols], edge_sb[:, cols], sw_all[:, cols], MULT)
-        for b in range(1, C // P):
+        for b in range(C // P):
             nc.sync.dma_start(x_tiles[b][:], x_blocks[b])
 
         for b in range(C // P):

@@ -1,6 +1,7 @@
 import math
 
 import concourse.mybir as mybir
+from concourse.masks import make_identity
 
 F32 = mybir.dt.float32
 BF16 = mybir.dt.bfloat16
@@ -14,7 +15,9 @@ E, N = 128, 4096
 NLOC, NNEI = 128, 32
 BANK = 512
 PIECE = 1024
-ATOMS = PIECE // NNEI
+BLOCKS = C // P
+PIECES = N // PIECE
+LEAD = 3
 
 FLOPS = 2 * C * E * N
 
@@ -28,47 +31,80 @@ def tile_repflowlayer_kernel(tc, x, edge, w_proj, sw, offs, out):
     with (
         tc.tile_pool(name="held", bufs=1) as held,
         tc.tile_pool(name="per_block", bufs=2) as per_block,
-        tc.tile_pool(name="per_piece", bufs=4) as per_piece,
-        tc.psum_pool(name="psum", bufs=8) as psum,
+        tc.tile_pool(name="per_piece", bufs=LEAD + 1) as per_piece,
+        tc.psum_pool(name="psum_p", bufs=4) as psum_p,
+        tc.psum_pool(name="psum_conv", bufs=2) as psum_conv,
     ):
         offsets = held.tile([P, N // 16], U16, name="offsets")
         w_sb = held.tile([E, C], BF16, name="w_sb")
         edge_sb = held.tile([E, N], BF16, name="edge_sb")
         sw_all = held.tile([E, N], F32, name="sw_all")
         edge_sw = held.tile([E, N], F32, name="edge_sw")
-        x_tiles = [held.tile([P, S], F32, name=f"x{b}") for b in range(C // P)]
+        identity = held.tile([P, P], F32, name="identity")
+        x_tiles = [held.tile([P, S], F32, name=f"x{b}") for b in range(BLOCKS)]
+
+        make_identity(nc, identity[:])
 
         nc.sync.dma_start(offsets[:], offs)
         nc.scalar.dma_start(w_sb[:], w_proj)
-        for k in range(N // PIECE):
+        for k in range(PIECES):
             cols = slice(k * PIECE, (k + 1) * PIECE)
             nc.sync.dma_start(sw_all[:, cols], sw_row[cols].partition_broadcast(E))
             nc.scalar.dma_start(edge_sb[:, cols], edge[:, cols])
             nc.vector.tensor_tensor(edge_sw[:, cols], edge_sb[:, cols], sw_all[:, cols], MULT)
-        for b in range(C // P):
+        for b in range(BLOCKS):
             nc.sync.dma_start(x_tiles[b][:], x_blocks[b])
 
-        for b in range(C // P):
-            x_blk = x_tiles[b]
-            w_blk = per_block.tile([E, P], F32, name="w_blk")
-            nc.scalar.mul(w_blk[:], w_sb[:, b * P : (b + 1) * P], 1.0 / (NNEI * math.sqrt(5.0)))
-            conv = per_block.tile([P, NLOC], F32, name="conv")
-            for k in range(N // PIECE):
-                p_sb = per_piece.tile([P, PIECE], F32, name="p_sb")
-                for h in range(PIECE // BANK):
-                    j0 = k * PIECE + h * BANK
-                    p_ps = psum.tile([P, BANK], F32, name="p_ps")
-                    nc.tensor.matmul(p_ps[:], w_blk[:], edge_sw[:, j0 : j0 + BANK], start=True, stop=True)
-                    nc.scalar.copy(p_sb[:, h * BANK : (h + 1) * BANK], p_ps[:])
-                msg = per_piece.tile([P, PIECE], F32, name="msg")
-                picked = x_blk[:].indirect(offsets[:, k * (PIECE // 16) : (k + 1) * (PIECE // 16)])
-                nc.vector.tensor_tensor(msg[:], picked, p_sb[:], MULT)
-                nc.vector.tensor_reduce(
-                    conv[:, k * ATOMS : (k + 1) * ATOMS],
-                    msg[:].rearrange("p (i t) -> p i t", t=NNEI),
-                    axis=mybir.AxisListType.X,
-                    op=ADD,
+        w_blks = {}
+        p_tiles = {}
+        msgs = {}
+
+        def project(b, k):
+            if k == 0:
+                w_blk = per_block.tile([E, P], F32, name="w_blk")
+                nc.scalar.mul(w_blk[:], w_sb[:, b * P : (b + 1) * P], 1.0 / (NNEI * math.sqrt(5.0)))
+                w_blks[b] = w_blk
+            p_sb = per_piece.tile([P, PIECE], F32, name="p_sb")
+            for h in range(PIECE // BANK):
+                j0 = k * PIECE + h * BANK
+                p_ps = psum_p.tile([P, BANK], F32, name="p_ps")
+                nc.tensor.matmul(p_ps[:], w_blks[b][:], edge_sw[:, j0 : j0 + BANK], start=True, stop=True)
+                nc.scalar.copy(p_sb[:, h * BANK : (h + 1) * BANK], p_ps[:])
+            p_tiles[(b, k)] = p_sb
+
+        def look_up(b, k):
+            if k == 0:
+                msgs[b] = per_block.tile([P, N], F32, name="msg")
+            picked = x_tiles[b][:].indirect(offsets[:, k * (PIECE // 16) : (k + 1) * (PIECE // 16)])
+            nc.vector.tensor_tensor(msgs[b][:, k * PIECE : (k + 1) * PIECE], picked, p_tiles[(b, k)][:], MULT)
+
+        def finish(b):
+            conv_t_ps = psum_conv.tile([NLOC, BANK], F32, name="conv_t_ps")
+            by_atom = msgs[b][:].rearrange("p (i t) -> p i t", t=NNEI)
+            for t in range(NNEI):
+                nc.tensor.matmul(
+                    conv_t_ps[:, 0:P],
+                    by_atom[:, :, t],
+                    identity[:],
+                    start=(t == 0),
+                    stop=(t == NNEI - 1),
+                    is_transpose=True,
                 )
+            conv_t = per_block.tile([NLOC, P], F32, name="conv_t")
+            nc.scalar.copy(conv_t[:], conv_t_ps[:, 0:P])
+            conv_ps = psum_conv.tile([P, BANK], F32, name="conv_ps")
+            nc.tensor.transpose(conv_ps[:, 0:NLOC], conv_t[:], identity[:])
             res = per_block.tile([P, NLOC], F32, name="res")
-            nc.vector.scalar_tensor_tensor(res[:], x_blk[:, 0:NLOC], 1.0 / math.sqrt(5.0), conv[:], MULT, ADD)
+            nc.vector.scalar_tensor_tensor(
+                res[:], x_tiles[b][:, 0:NLOC], 1.0 / math.sqrt(5.0), conv_ps[:, 0:NLOC], MULT, ADD
+            )
             nc.sync.dma_start(out_blocks[b], res[:])
+
+        for n in range(BLOCKS * PIECES + LEAD):
+            if n < BLOCKS * PIECES:
+                project(n // PIECES, n % PIECES)
+            if n >= LEAD:
+                b, k = (n - LEAD) // PIECES, (n - LEAD) % PIECES
+                look_up(b, k)
+                if k == PIECES - 1:
+                    finish(b)

@@ -7,7 +7,6 @@ F32 = mybir.dt.float32
 BF16 = mybir.dt.bfloat16
 U16 = mybir.dt.uint16
 MULT = mybir.AluOpType.mult
-ADD = mybir.AluOpType.add
 
 P = 128
 C, S = 1024, 2048
@@ -17,7 +16,9 @@ BANK = 512
 PIECE = 1024
 BLOCKS = C // P
 PIECES = N // PIECE
+STEPS = BLOCKS * PIECES
 LEAD = 3
+SHARE = NNEI // PIECES
 
 FLOPS = 2 * C * E * N
 
@@ -30,7 +31,7 @@ def tile_repflowlayer_kernel(tc, x, edge, w_proj, sw, offs, out):
 
     with (
         tc.tile_pool(name="held", bufs=1) as held,
-        tc.tile_pool(name="per_block", bufs=2) as per_block,
+        tc.tile_pool(name="per_block", bufs=3) as per_block,
         tc.tile_pool(name="per_piece", bufs=LEAD + 1) as per_piece,
         tc.psum_pool(name="psum_p", bufs=4) as psum_p,
         tc.psum_pool(name="psum_conv", bufs=2) as psum_conv,
@@ -55,22 +56,18 @@ def tile_repflowlayer_kernel(tc, x, edge, w_proj, sw, offs, out):
         for b in range(BLOCKS):
             nc.sync.dma_start(x_tiles[b][:], x_blocks[b])
 
-        w_blks = {}
-        p_tiles = {}
-        msgs = {}
+        w_blks, p_tiles, msgs, sums_ps, sums_sb, results_ps = {}, {}, {}, {}, {}, {}
 
         def project(b, k):
             if k == 0:
-                w_blk = per_block.tile([E, P], F32, name="w_blk")
-                nc.scalar.mul(w_blk[:], w_sb[:, b * P : (b + 1) * P], 1.0 / (NNEI * math.sqrt(5.0)))
-                w_blks[b] = w_blk
-            p_sb = per_piece.tile([P, PIECE], F32, name="p_sb")
+                w_blks[b] = per_block.tile([E, P], F32, name="w_blk")
+                nc.scalar.mul(w_blks[b][:], w_sb[:, b * P : (b + 1) * P], 1.0 / NNEI)
+            p_tiles[(b, k)] = per_piece.tile([P, PIECE], F32, name="p_sb")
             for h in range(PIECE // BANK):
                 j0 = k * PIECE + h * BANK
                 p_ps = psum_p.tile([P, BANK], F32, name="p_ps")
                 nc.tensor.matmul(p_ps[:], w_blks[b][:], edge_sw[:, j0 : j0 + BANK], start=True, stop=True)
-                nc.scalar.copy(p_sb[:, h * BANK : (h + 1) * BANK], p_ps[:])
-            p_tiles[(b, k)] = p_sb
+                nc.scalar.copy(p_tiles[(b, k)][:, h * BANK : (h + 1) * BANK], p_ps[:])
 
         def look_up(b, k):
             if k == 0:
@@ -78,33 +75,40 @@ def tile_repflowlayer_kernel(tc, x, edge, w_proj, sw, offs, out):
             picked = x_tiles[b][:].indirect(offsets[:, k * (PIECE // 16) : (k + 1) * (PIECE // 16)])
             nc.vector.tensor_tensor(msgs[b][:, k * PIECE : (k + 1) * PIECE], picked, p_tiles[(b, k)][:], MULT)
 
-        def finish(b):
-            conv_t_ps = psum_conv.tile([NLOC, BANK], F32, name="conv_t_ps")
-            by_atom = msgs[b][:].rearrange("p (i t) -> p i t", t=NNEI)
-            for t in range(NNEI):
+        def add_up(b, share):
+            def add_transposed(columns, start, stop):
                 nc.tensor.matmul(
-                    conv_t_ps[:, 0:P],
-                    by_atom[:, :, t],
-                    identity[:],
-                    start=(t == 0),
-                    stop=(t == NNEI - 1),
-                    is_transpose=True,
+                    sums_ps[b][:, 0:P], columns, identity[:], start=start, stop=stop, is_transpose=True
                 )
-            conv_t = per_block.tile([NLOC, P], F32, name="conv_t")
-            nc.scalar.copy(conv_t[:], conv_t_ps[:, 0:P])
-            conv_ps = psum_conv.tile([P, BANK], F32, name="conv_ps")
-            nc.tensor.transpose(conv_ps[:, 0:NLOC], conv_t[:], identity[:])
-            res = per_block.tile([P, NLOC], F32, name="res")
-            nc.vector.scalar_tensor_tensor(
-                res[:], x_tiles[b][:, 0:NLOC], 1.0 / math.sqrt(5.0), conv_ps[:, 0:NLOC], MULT, ADD
-            )
-            nc.sync.dma_start(out_blocks[b], res[:])
 
-        for n in range(BLOCKS * PIECES + LEAD):
-            if n < BLOCKS * PIECES:
+            if share == 0:
+                sums_ps[b] = psum_conv.tile([NLOC, BANK], F32, name="sums_ps")
+                add_transposed(x_tiles[b][:, 0:NLOC], True, False)
+            by_atom = msgs[b][:].rearrange("p (i t) -> p i t", t=NNEI)
+            for t in range(share * SHARE, (share + 1) * SHARE):
+                add_transposed(by_atom[:, :, t], False, t == NNEI - 1)
+
+        def scale(b):
+            sums_sb[b] = per_block.tile([NLOC, P], F32, name="sums_sb")
+            nc.scalar.mul(sums_sb[b][:], sums_ps[b][:, 0:P], 1.0 / math.sqrt(5.0))
+
+        def turn_back(b):
+            results_ps[b] = psum_conv.tile([P, BANK], F32, name="result_ps")
+            nc.tensor.transpose(results_ps[b][:, 0:NLOC], sums_sb[b][:], identity[:])
+
+        def store(b):
+            result = per_block.tile([P, NLOC], F32, name="result")
+            nc.scalar.copy(result[:], results_ps[b][:, 0:NLOC])
+            nc.sync.dma_start(out_blocks[b], result[:])
+
+        after = [lambda b, share=share: add_up(b, share) for share in range(PIECES)] + [scale, turn_back, store]
+
+        for n in range(STEPS + LEAD + len(after)):
+            if n < STEPS:
                 project(n // PIECES, n % PIECES)
-            if n >= LEAD:
-                b, k = (n - LEAD) // PIECES, (n - LEAD) % PIECES
-                look_up(b, k)
-                if k == PIECES - 1:
-                    finish(b)
+            if 0 <= n - LEAD < STEPS:
+                look_up((n - LEAD) // PIECES, (n - LEAD) % PIECES)
+            for turn, entry in enumerate(after):
+                b, k = divmod(n - LEAD - turn, PIECES)
+                if k == PIECES - 1 and 0 <= b < BLOCKS:
+                    entry(b)

@@ -7,6 +7,7 @@ F32 = mybir.dt.float32
 BF16 = mybir.dt.bfloat16
 U16 = mybir.dt.uint16
 MULT = mybir.AluOpType.mult
+SUBTRACT = mybir.AluOpType.subtract
 
 P = 128
 C, S = 1024, 2048
@@ -41,6 +42,8 @@ def tile_repflowlayer_kernel(tc, x, edge, w_proj, sw, offs, out):
         edge_sb = held.tile([E, N], BF16, name="edge_sb")
         sw_all = held.tile([E, N], F32, name="sw_all")
         edge_sw = held.tile([E, N], F32, name="edge_sw")
+        left = held.tile([E, N], F32, name="left")
+        terms = [held.tile([E, N], BF16, name=f"term{i}") for i in range(3)]
         identity = held.tile([P, P], F32, name="identity")
         x_tiles = [held.tile([P, S], F32, name=f"x{b}") for b in range(BLOCKS)]
 
@@ -52,22 +55,35 @@ def tile_repflowlayer_kernel(tc, x, edge, w_proj, sw, offs, out):
             cols = slice(k * PIECE, (k + 1) * PIECE)
             nc.sync.dma_start(sw_all[:, cols], sw_row[cols].partition_broadcast(E))
             nc.scalar.dma_start(edge_sb[:, cols], edge[:, cols])
-            nc.vector.tensor_tensor(edge_sw[:, cols], edge_sb[:, cols], sw_all[:, cols], MULT)
         for b in range(BLOCKS):
             nc.sync.dma_start(x_tiles[b][:], x_blocks[b])
 
-        w_blks, p_tiles, msgs, sums_ps, sums_sb, results_ps = {}, {}, {}, {}, {}, {}
+        pieces = [slice(k * PIECE, (k + 1) * PIECE) for k in range(PIECES)]
+        for cols in pieces:
+            nc.vector.tensor_tensor(edge_sw[:, cols], edge_sb[:, cols], sw_all[:, cols], MULT)
+            nc.scalar.copy(terms[0][:, cols], edge_sw[:, cols])
+        for cols in pieces:
+            nc.vector.tensor_tensor(left[:, cols], edge_sw[:, cols], terms[0][:, cols], SUBTRACT)
+            nc.scalar.copy(terms[1][:, cols], left[:, cols])
+        for cols in pieces:
+            nc.vector.tensor_tensor(terms[2][:, cols], left[:, cols], terms[1][:, cols], SUBTRACT)
+
+        p_tiles, msgs, sums_ps, sums_sb, results_ps = {}, {}, {}, {}, {}
 
         def project(b, k):
-            if k == 0:
-                w_blks[b] = per_block.tile([E, P], F32, name="w_blk")
-                nc.scalar.mul(w_blks[b][:], w_sb[:, b * P : (b + 1) * P], 1.0 / NNEI)
             p_tiles[(b, k)] = per_piece.tile([P, PIECE], F32, name="p_sb")
             for h in range(PIECE // BANK):
                 j0 = k * PIECE + h * BANK
                 p_ps = psum_p.tile([P, BANK], F32, name="p_ps")
-                nc.tensor.matmul(p_ps[:], w_blks[b][:], edge_sw[:, j0 : j0 + BANK], start=True, stop=True)
-                nc.scalar.copy(p_tiles[(b, k)][:, h * BANK : (h + 1) * BANK], p_ps[:])
+                for i, term in enumerate(terms):
+                    nc.tensor.matmul(
+                        p_ps[:],
+                        w_sb[:, b * P : (b + 1) * P],
+                        term[:, j0 : j0 + BANK],
+                        start=(i == 0),
+                        stop=(i == len(terms) - 1),
+                    )
+                nc.scalar.mul(p_tiles[(b, k)][:, h * BANK : (h + 1) * BANK], p_ps[:], 1.0 / NNEI)
 
         def look_up(b, k):
             if k == 0:

@@ -18,8 +18,9 @@ PIECE = 1024
 BLOCKS = C // P
 PIECES = N // PIECE
 STEPS = BLOCKS * PIECES
-LEAD = 3
+LEAD = 5
 SHARE = NNEI // PIECES
+PLAIN = 1
 
 FLOPS = 2 * C * E * N
 
@@ -39,6 +40,7 @@ def tile_repflowlayer_kernel(tc, x, edge, w_proj, sw, offs, out):
     ):
         offsets = held.tile([P, N // 16], U16, name="offsets")
         w_sb = held.tile([E, C], BF16, name="w_sb")
+        w_f32 = held.tile([E, C], F32, name="w_f32")
         edge_sb = held.tile([E, N], BF16, name="edge_sb")
         sw_all = held.tile([E, N], F32, name="sw_all")
         edge_sw = held.tile([E, N], F32, name="edge_sw")
@@ -49,24 +51,33 @@ def tile_repflowlayer_kernel(tc, x, edge, w_proj, sw, offs, out):
 
         make_identity(nc, identity[:])
 
-        nc.sync.dma_start(offsets[:], offs)
-        nc.scalar.dma_start(w_sb[:], w_proj)
         for k in range(PIECES):
             cols = slice(k * PIECE, (k + 1) * PIECE)
             nc.sync.dma_start(sw_all[:, cols], sw_row[cols].partition_broadcast(E))
             nc.scalar.dma_start(edge_sb[:, cols], edge[:, cols])
+            if k == 0:
+                nc.scalar.dma_start(w_sb[:], w_proj)
+        nc.sync.dma_start(offsets[:], offs)
         for b in range(BLOCKS):
             nc.sync.dma_start(x_tiles[b][:], x_blocks[b])
 
-        pieces = [slice(k * PIECE, (k + 1) * PIECE) for k in range(PIECES)]
-        for cols in pieces:
-            nc.vector.tensor_tensor(edge_sw[:, cols], edge_sb[:, cols], sw_all[:, cols], MULT)
-            nc.scalar.copy(terms[0][:, cols], edge_sw[:, cols])
-        for cols in pieces:
-            nc.vector.tensor_tensor(left[:, cols], edge_sw[:, cols], terms[0][:, cols], SUBTRACT)
-            nc.scalar.copy(terms[1][:, cols], left[:, cols])
-        for cols in pieces:
-            nc.vector.tensor_tensor(terms[2][:, cols], left[:, cols], terms[1][:, cols], SUBTRACT)
+        def cols_of(k):
+            return slice(k * PIECE, (k + 1) * PIECE)
+
+        nc.scalar.copy(w_f32[:], w_sb[:])
+        for k in range(PIECES + 2):
+            if k < PIECES:
+                cols = cols_of(k)
+                nc.vector.tensor_tensor(edge_sw[:, cols], edge_sb[:, cols], sw_all[:, cols], MULT)
+            if PLAIN <= k < PIECES:
+                nc.scalar.copy(terms[0][:, cols], edge_sw[:, cols])
+            if PLAIN <= k - 1 < PIECES:
+                cols = cols_of(k - 1)
+                nc.vector.tensor_tensor(left[:, cols], edge_sw[:, cols], terms[0][:, cols], SUBTRACT)
+                nc.scalar.copy(terms[1][:, cols], left[:, cols])
+            if PLAIN <= k - 2 < PIECES:
+                cols = cols_of(k - 2)
+                nc.vector.tensor_tensor(terms[2][:, cols], left[:, cols], terms[1][:, cols], SUBTRACT)
 
         p_tiles, msgs, sums_ps, sums_sb, results_ps = {}, {}, {}, {}, {}
 
@@ -75,13 +86,14 @@ def tile_repflowlayer_kernel(tc, x, edge, w_proj, sw, offs, out):
             for h in range(PIECE // BANK):
                 j0 = k * PIECE + h * BANK
                 p_ps = psum_p.tile([P, BANK], F32, name="p_ps")
-                for i, term in enumerate(terms):
+                passes = [(w_f32, edge_sw)] if k < PLAIN else [(w_sb, term) for term in terms]
+                for i, (weights, moving) in enumerate(passes):
                     nc.tensor.matmul(
                         p_ps[:],
-                        w_sb[:, b * P : (b + 1) * P],
-                        term[:, j0 : j0 + BANK],
+                        weights[:, b * P : (b + 1) * P],
+                        moving[:, j0 : j0 + BANK],
                         start=(i == 0),
-                        stop=(i == len(terms) - 1),
+                        stop=(i == len(passes) - 1),
                     )
                 nc.scalar.mul(p_tiles[(b, k)][:, h * BANK : (h + 1) * BANK], p_ps[:], 1.0 / NNEI)
 

@@ -7,6 +7,7 @@ F32 = mybir.dt.float32
 BF16 = mybir.dt.bfloat16
 U16 = mybir.dt.uint16
 MULT = mybir.AluOpType.mult
+ADD = mybir.AluOpType.add
 SUBTRACT = mybir.AluOpType.subtract
 
 P = 128
@@ -129,14 +130,27 @@ def tile_repflowlayer_kernel(tc, x, edge, w_proj, sw, offs, out):
             nc.scalar.copy(result[:], results_ps[b][:, 0:NLOC])
             nc.sync.dma_start(out_blocks[b], result[:])
 
+        def finish_on_vector(b):
+            own = per_block.tile([P, NLOC], F32, name="own")
+            nc.scalar.mul(own[:], x_tiles[b][:, 0:NLOC], 1.0 / math.sqrt(5.0))
+            sums = per_block.tile([P, NLOC], F32, name="sums")
+            nc.vector.tensor_reduce(
+                sums[:], msgs[b][:].rearrange("p (i t) -> p i t", t=NNEI), axis=mybir.AxisListType.X, op=ADD
+            )
+            result = per_block.tile([P, NLOC], F32, name="result")
+            nc.vector.scalar_tensor_tensor(result[:], sums[:], 1.0 / math.sqrt(5.0), own[:], MULT, ADD)
+            nc.sync.dma_start(out_blocks[b], result[:])
+
         after = [lambda b, share=share: add_up(b, share) for share in range(PIECES)] + [scale, turn_back, store]
 
-        for n in range(STEPS + LEAD + len(after)):
+        for n in range(STEPS + LEAD + len(after) - PIECES):
             if n < STEPS:
                 project(n // PIECES, n % PIECES)
             if 0 <= n - LEAD < STEPS:
                 look_up((n - LEAD) // PIECES, (n - LEAD) % PIECES)
             for turn, entry in enumerate(after):
                 b, k = divmod(n - LEAD - turn, PIECES)
-                if k == PIECES - 1 and 0 <= b < BLOCKS:
+                if k == PIECES - 1 and 0 <= b < BLOCKS - 1:
                     entry(b)
+            if n - LEAD == STEPS - 1:
+                finish_on_vector(BLOCKS - 1)

@@ -9,6 +9,7 @@ U16 = mybir.dt.uint16
 MULT = mybir.AluOpType.mult
 ADD = mybir.AluOpType.add
 SUBTRACT = mybir.AluOpType.subtract
+COPY = mybir.ActivationFunctionType.Copy
 
 P = 128
 C, S = 1024, 2048
@@ -21,7 +22,8 @@ PIECES = N // PIECE
 STEPS = BLOCKS * PIECES
 LEAD = 5
 SHARE = NNEI // PIECES
-PLAIN = 1
+GROUPS = BANK // P
+SPLIT_PIECES = [k for k in range(PIECES) if k % 2 == 1]
 
 FLOPS = 2 * C * E * N
 
@@ -36,73 +38,114 @@ def tile_repflowlayer_kernel(tc, x, edge, w_proj, sw, offs, out):
         tc.tile_pool(name="held", bufs=1) as held,
         tc.tile_pool(name="per_block", bufs=3) as per_block,
         tc.tile_pool(name="per_piece", bufs=LEAD + 1) as per_piece,
-        tc.psum_pool(name="psum_p", bufs=4) as psum_p,
-        tc.psum_pool(name="psum_conv", bufs=2) as psum_conv,
+        tc.tile_pool(name="turned", bufs=2) as turned,
+        tc.psum_pool(name="psum_turned", bufs=2) as psum_turned,
+        tc.psum_pool(name="psum_p", bufs=3) as psum_p,
+        tc.psum_pool(name="psum_sums", bufs=2) as psum_sums,
+        tc.psum_pool(name="psum_result", bufs=1) as psum_result,
     ):
         offsets = held.tile([P, N // 16], U16, name="offsets")
         w_sb = held.tile([E, C], BF16, name="w_sb")
-        w_f32 = held.tile([E, C], F32, name="w_f32")
         edge_sb = held.tile([E, N], BF16, name="edge_sb")
-        sw_all = held.tile([E, N], F32, name="sw_all")
-        edge_sw = held.tile([E, N], F32, name="edge_sw")
-        left = held.tile([E, N], F32, name="left")
-        terms = [held.tile([E, N], BF16, name=f"term{i}") for i in range(3)]
+        sw_col = held.tile([P, N // P], F32, name="sw_col")
+        width = len(SPLIT_PIECES) * PIECE
+        sw_all = held.tile([E, width], F32, name="sw_all")
+        edge_sw = held.tile([E, width], F32, name="edge_sw")
+        left = held.tile([E, width], F32, name="left")
+        terms = [held.tile([E, width], BF16, name=f"term{i}") for i in range(3)]
         identity = held.tile([P, P], F32, name="identity")
         x_tiles = [held.tile([P, S], F32, name=f"x{b}") for b in range(BLOCKS)]
 
         make_identity(nc, identity[:])
 
-        for k in range(PIECES):
-            cols = slice(k * PIECE, (k + 1) * PIECE)
-            nc.sync.dma_start(sw_all[:, cols], sw_row[cols].partition_broadcast(E))
-            nc.scalar.dma_start(edge_sb[:, cols], edge[:, cols])
+        def in_list(k):
+            return slice(k * PIECE, (k + 1) * PIECE)
+
+        def in_split(k):
+            return slice(SPLIT_PIECES.index(k) * PIECE, (SPLIT_PIECES.index(k) + 1) * PIECE)
+
+        for k in SPLIT_PIECES + [k for k in range(PIECES) if k not in SPLIT_PIECES]:
+            nc.scalar.dma_start(edge_sb[:, in_list(k)], edge[:, in_list(k)])
             if k == 0:
                 nc.scalar.dma_start(w_sb[:], w_proj)
+            if k in SPLIT_PIECES:
+                nc.sync.dma_start(sw_all[:, in_split(k)], sw_row[in_list(k)].partition_broadcast(E))
+            else:
+                with nc.allow_non_contiguous_dma(reason="one value of sw to a partition"):
+                    nc.sync.dma_start(
+                        sw_col[:, k * (PIECE // P) : (k + 1) * (PIECE // P)],
+                        sw_row[in_list(k)].rearrange("(g p) -> p g", p=P),
+                    )
         nc.sync.dma_start(offsets[:], offs)
         for b in range(BLOCKS):
             nc.sync.dma_start(x_tiles[b][:], x_blocks[b])
 
-        def cols_of(k):
-            return slice(k * PIECE, (k + 1) * PIECE)
-
-        nc.scalar.copy(w_f32[:], w_sb[:])
-        for k in range(PIECES + 2):
-            if k < PIECES:
-                cols = cols_of(k)
-                nc.vector.tensor_tensor(edge_sw[:, cols], edge_sb[:, cols], sw_all[:, cols], MULT)
-            if PLAIN <= k < PIECES:
+        halves = [(k * PIECE + h, in_split(k).start + h) for k in SPLIT_PIECES for h in (0, PIECE // 2)]
+        for r in range(len(halves) + 2):
+            if r < len(halves):
+                j0, s0 = halves[r]
+                cols = slice(s0, s0 + PIECE // 2)
+                nc.vector.tensor_tensor(edge_sw[:, cols], edge_sb[:, j0 : j0 + PIECE // 2], sw_all[:, cols], MULT)
                 nc.scalar.copy(terms[0][:, cols], edge_sw[:, cols])
-            if PLAIN <= k - 1 < PIECES:
-                cols = cols_of(k - 1)
+            if 0 <= r - 1 < len(halves):
+                cols = slice(halves[r - 1][1], halves[r - 1][1] + PIECE // 2)
                 nc.vector.tensor_tensor(left[:, cols], edge_sw[:, cols], terms[0][:, cols], SUBTRACT)
                 nc.scalar.copy(terms[1][:, cols], left[:, cols])
-            if PLAIN <= k - 2 < PIECES:
-                cols = cols_of(k - 2)
+            if 0 <= r - 2 < len(halves):
+                cols = slice(halves[r - 2][1], halves[r - 2][1] + PIECE // 2)
                 nc.vector.tensor_tensor(terms[2][:, cols], left[:, cols], terms[1][:, cols], SUBTRACT)
 
-        p_tiles, msgs, sums_ps, sums_sb, results_ps = {}, {}, {}, {}, {}
+        turned_tiles, p_tiles, msgs, sums_ps, sums_sb, results_ps = {}, {}, {}, {}, {}, {}
 
-        def project(b, k):
+        def project_turned(b, k):
+            turned_tiles[(b, k)] = turned.tile([P, PIECE], F32, name="turned_sb")
+            for h in range(PIECE // BANK):
+                turned_ps = psum_turned.tile([P, BANK], F32, name="turned_ps")
+                for g in range(GROUPS):
+                    j0 = k * PIECE + h * BANK + g * P
+                    nc.tensor.matmul(
+                        turned_ps[:, g * P : (g + 1) * P],
+                        edge_sb[:, j0 : j0 + P],
+                        w_sb[:, b * P : (b + 1) * P],
+                        start=True,
+                        stop=True,
+                    )
+                for g in range(GROUPS):
+                    j0 = k * PIECE + h * BANK + g * P
+                    nc.scalar.activation(
+                        turned_tiles[(b, k)][:, j0 % PIECE : j0 % PIECE + P],
+                        turned_ps[:, g * P : (g + 1) * P],
+                        COPY,
+                        scale=sw_col[:, j0 // P : j0 // P + 1],
+                    )
+
+        def finish_p(b, k):
             p_tiles[(b, k)] = per_piece.tile([P, PIECE], F32, name="p_sb")
             for h in range(PIECE // BANK):
-                j0 = k * PIECE + h * BANK
                 p_ps = psum_p.tile([P, BANK], F32, name="p_ps")
-                passes = [(w_f32, edge_sw)] if k < PLAIN else [(w_sb, term) for term in terms]
-                for i, (weights, moving) in enumerate(passes):
-                    nc.tensor.matmul(
-                        p_ps[:],
-                        weights[:, b * P : (b + 1) * P],
-                        moving[:, j0 : j0 + BANK],
-                        start=(i == 0),
-                        stop=(i == len(passes) - 1),
-                    )
+                if k in SPLIT_PIECES:
+                    j0 = in_split(k).start + h * BANK
+                    for i, term in enumerate(terms):
+                        nc.tensor.matmul(
+                            p_ps[:],
+                            w_sb[:, b * P : (b + 1) * P],
+                            term[:, j0 : j0 + BANK],
+                            start=(i == 0),
+                            stop=(i == len(terms) - 1),
+                        )
+                else:
+                    for g in range(GROUPS):
+                        j0 = h * BANK + g * P
+                        nc.tensor.transpose(
+                            p_ps[:, g * P : (g + 1) * P], turned_tiles[(b, k)][:, j0 : j0 + P], identity[:]
+                        )
                 nc.scalar.mul(p_tiles[(b, k)][:, h * BANK : (h + 1) * BANK], p_ps[:], 1.0 / NNEI)
 
         def look_up(b, k):
             if k == 0:
                 msgs[b] = per_block.tile([P, N], F32, name="msg")
             picked = x_tiles[b][:].indirect(offsets[:, k * (PIECE // 16) : (k + 1) * (PIECE // 16)])
-            nc.vector.tensor_tensor(msgs[b][:, k * PIECE : (k + 1) * PIECE], picked, p_tiles[(b, k)][:], MULT)
+            nc.vector.tensor_tensor(msgs[b][:, in_list(k)], picked, p_tiles[(b, k)][:], MULT)
 
         def add_up(b, share):
             def add_transposed(columns, start, stop):
@@ -111,7 +154,7 @@ def tile_repflowlayer_kernel(tc, x, edge, w_proj, sw, offs, out):
                 )
 
             if share == 0:
-                sums_ps[b] = psum_conv.tile([NLOC, BANK], F32, name="sums_ps")
+                sums_ps[b] = psum_sums.tile([NLOC, BANK], F32, name="sums_ps")
                 add_transposed(x_tiles[b][:, 0:NLOC], True, False)
             by_atom = msgs[b][:].rearrange("p (i t) -> p i t", t=NNEI)
             for t in range(share * SHARE, (share + 1) * SHARE):
@@ -122,7 +165,7 @@ def tile_repflowlayer_kernel(tc, x, edge, w_proj, sw, offs, out):
             nc.scalar.mul(sums_sb[b][:], sums_ps[b][:, 0:P], 1.0 / math.sqrt(5.0))
 
         def turn_back(b):
-            results_ps[b] = psum_conv.tile([P, BANK], F32, name="result_ps")
+            results_ps[b] = psum_result.tile([P, BANK], F32, name="result_ps")
             nc.tensor.transpose(results_ps[b][:, 0:NLOC], sums_sb[b][:], identity[:])
 
         def store(b):
@@ -131,9 +174,9 @@ def tile_repflowlayer_kernel(tc, x, edge, w_proj, sw, offs, out):
             nc.sync.dma_start(out_blocks[b], result[:])
 
         def finish_on_vector(b):
-            own = per_block.tile([P, NLOC], F32, name="own")
+            own = held.tile([P, NLOC], F32, name="own")
             nc.scalar.mul(own[:], x_tiles[b][:, 0:NLOC], 1.0 / math.sqrt(5.0))
-            sums = per_block.tile([P, NLOC], F32, name="sums")
+            sums = held.tile([P, NLOC], F32, name="sums")
             nc.vector.tensor_reduce(
                 sums[:], msgs[b][:].rearrange("p (i t) -> p i t", t=NNEI), axis=mybir.AxisListType.X, op=ADD
             )
@@ -143,14 +186,17 @@ def tile_repflowlayer_kernel(tc, x, edge, w_proj, sw, offs, out):
 
         after = [lambda b, share=share: add_up(b, share) for share in range(PIECES)] + [scale, turn_back, store]
 
-        for n in range(STEPS + LEAD + len(after) - PIECES):
-            if n < STEPS:
-                project(n // PIECES, n % PIECES)
-            if 0 <= n - LEAD < STEPS:
-                look_up((n - LEAD) // PIECES, (n - LEAD) % PIECES)
+        for n in range(STEPS + 1 + LEAD + len(after) - PIECES):
+            if n < STEPS and n % PIECES not in SPLIT_PIECES:
+                project_turned(n // PIECES, n % PIECES)
+            if 0 <= n - 1 < STEPS:
+                finish_p((n - 1) // PIECES, (n - 1) % PIECES)
+            m = n - 1 - LEAD
+            if 0 <= m < STEPS:
+                look_up(m // PIECES, m % PIECES)
             for turn, entry in enumerate(after):
-                b, k = divmod(n - LEAD - turn, PIECES)
+                b, k = divmod(m - turn, PIECES)
                 if k == PIECES - 1 and 0 <= b < BLOCKS - 1:
                     entry(b)
-            if n - LEAD == STEPS - 1:
+            if m == STEPS - 1:
                 finish_on_vector(BLOCKS - 1)

@@ -23,7 +23,7 @@ STEPS = BLOCKS * PIECES
 LEAD = 5
 SHARE = NNEI // PIECES
 GROUPS = BANK // P
-SPLIT_PIECES = [k for k in range(PIECES) if k % 2 == 1]
+SPLIT_PIECES = [PIECES - 1]
 
 FLOPS = 2 * C * E * N
 

@@ -8,7 +8,6 @@ BF16 = mybir.dt.bfloat16
 U16 = mybir.dt.uint16
 MULT = mybir.AluOpType.mult
 ADD = mybir.AluOpType.add
-SUBTRACT = mybir.AluOpType.subtract
 COPY = mybir.ActivationFunctionType.Copy
 
 P = 128
@@ -23,7 +22,6 @@ STEPS = BLOCKS * PIECES
 LEAD = 5
 SHARE = NNEI // PIECES
 GROUPS = BANK // P
-SPLIT_PIECES = [PIECES - 1]
 
 FLOPS = 2 * C * E * N
 
@@ -48,11 +46,6 @@ def tile_repflowlayer_kernel(tc, x, edge, w_proj, sw, offs, out):
         w_sb = held.tile([E, C], BF16, name="w_sb")
         edge_sb = held.tile([E, N], BF16, name="edge_sb")
         sw_col = held.tile([P, N // P], F32, name="sw_col")
-        width = len(SPLIT_PIECES) * PIECE
-        sw_all = held.tile([E, width], F32, name="sw_all")
-        edge_sw = held.tile([E, width], F32, name="edge_sw")
-        left = held.tile([E, width], F32, name="left")
-        terms = [held.tile([E, width], BF16, name=f"term{i}") for i in range(3)]
         identity = held.tile([P, P], F32, name="identity")
         x_tiles = [held.tile([P, S], F32, name=f"x{b}") for b in range(BLOCKS)]
 
@@ -61,39 +54,24 @@ def tile_repflowlayer_kernel(tc, x, edge, w_proj, sw, offs, out):
         def in_list(k):
             return slice(k * PIECE, (k + 1) * PIECE)
 
-        def in_split(k):
-            return slice(SPLIT_PIECES.index(k) * PIECE, (SPLIT_PIECES.index(k) + 1) * PIECE)
+        def load_switch(k):
+            with nc.allow_non_contiguous_dma(reason="one value of sw to a partition"):
+                nc.sync.dma_start(
+                    sw_col[:, k * (PIECE // P) : (k + 1) * (PIECE // P)],
+                    sw_row[in_list(k)].rearrange("(g p) -> p g", p=P),
+                )
 
-        for k in SPLIT_PIECES + [k for k in range(PIECES) if k not in SPLIT_PIECES]:
+        load_switch(0)
+        nc.sync.dma_start(offsets[:], offs)
+        nc.sync.dma_start(x_tiles[0][:], x_blocks[0])
+        for k in range(PIECES):
             nc.scalar.dma_start(edge_sb[:, in_list(k)], edge[:, in_list(k)])
             if k == 0:
                 nc.scalar.dma_start(w_sb[:], w_proj)
-            if k in SPLIT_PIECES:
-                nc.sync.dma_start(sw_all[:, in_split(k)], sw_row[in_list(k)].partition_broadcast(E))
             else:
-                with nc.allow_non_contiguous_dma(reason="one value of sw to a partition"):
-                    nc.sync.dma_start(
-                        sw_col[:, k * (PIECE // P) : (k + 1) * (PIECE // P)],
-                        sw_row[in_list(k)].rearrange("(g p) -> p g", p=P),
-                    )
-        nc.sync.dma_start(offsets[:], offs)
-        for b in range(BLOCKS):
+                load_switch(k)
+        for b in range(1, BLOCKS):
             nc.sync.dma_start(x_tiles[b][:], x_blocks[b])
-
-        halves = [(k * PIECE + h, in_split(k).start + h) for k in SPLIT_PIECES for h in (0, PIECE // 2)]
-        for r in range(len(halves) + 2):
-            if r < len(halves):
-                j0, s0 = halves[r]
-                cols = slice(s0, s0 + PIECE // 2)
-                nc.vector.tensor_tensor(edge_sw[:, cols], edge_sb[:, j0 : j0 + PIECE // 2], sw_all[:, cols], MULT)
-                nc.scalar.copy(terms[0][:, cols], edge_sw[:, cols])
-            if 0 <= r - 1 < len(halves):
-                cols = slice(halves[r - 1][1], halves[r - 1][1] + PIECE // 2)
-                nc.vector.tensor_tensor(left[:, cols], edge_sw[:, cols], terms[0][:, cols], SUBTRACT)
-                nc.scalar.copy(terms[1][:, cols], left[:, cols])
-            if 0 <= r - 2 < len(halves):
-                cols = slice(halves[r - 2][1], halves[r - 2][1] + PIECE // 2)
-                nc.vector.tensor_tensor(terms[2][:, cols], left[:, cols], terms[1][:, cols], SUBTRACT)
 
         turned_tiles, p_tiles, msgs, sums_ps, sums_sb, results_ps = {}, {}, {}, {}, {}, {}
 
@@ -123,22 +101,11 @@ def tile_repflowlayer_kernel(tc, x, edge, w_proj, sw, offs, out):
             p_tiles[(b, k)] = per_piece.tile([P, PIECE], F32, name="p_sb")
             for h in range(PIECE // BANK):
                 p_ps = psum_p.tile([P, BANK], F32, name="p_ps")
-                if k in SPLIT_PIECES:
-                    j0 = in_split(k).start + h * BANK
-                    for i, term in enumerate(terms):
-                        nc.tensor.matmul(
-                            p_ps[:],
-                            w_sb[:, b * P : (b + 1) * P],
-                            term[:, j0 : j0 + BANK],
-                            start=(i == 0),
-                            stop=(i == len(terms) - 1),
-                        )
-                else:
-                    for g in range(GROUPS):
-                        j0 = h * BANK + g * P
-                        nc.tensor.transpose(
-                            p_ps[:, g * P : (g + 1) * P], turned_tiles[(b, k)][:, j0 : j0 + P], identity[:]
-                        )
+                for g in range(GROUPS):
+                    j0 = h * BANK + g * P
+                    nc.tensor.transpose(
+                        p_ps[:, g * P : (g + 1) * P], turned_tiles[(b, k)][:, j0 : j0 + P], identity[:]
+                    )
                 nc.scalar.mul(p_tiles[(b, k)][:, h * BANK : (h + 1) * BANK], p_ps[:], 1.0 / NNEI)
 
         def look_up(b, k):
@@ -187,7 +154,7 @@ def tile_repflowlayer_kernel(tc, x, edge, w_proj, sw, offs, out):
         after = [lambda b, share=share: add_up(b, share) for share in range(PIECES)] + [scale, turn_back, store]
 
         for n in range(STEPS + 1 + LEAD + len(after) - PIECES):
-            if n < STEPS and n % PIECES not in SPLIT_PIECES:
+            if n < STEPS:
                 project_turned(n // PIECES, n % PIECES)
             if 0 <= n - 1 < STEPS:
                 finish_p((n - 1) // PIECES, (n - 1) % PIECES)

@@ -17,11 +17,17 @@ NLOC, NNEI = 128, 32
 BANK = 512
 PIECE = 1024
 BLOCKS = C // P
-PIECES = N // PIECE
-STEPS = BLOCKS * PIECES
-LEAD = 5
-SHARE = NNEI // PIECES
-GROUPS = BANK // P
+GROUPS = N // P
+BLOCK = 32
+QUARTERS = P // BLOCK
+UNIT_GROUPS = BANK // P
+UNITS = N // BANK
+STEPS = BLOCKS * UNITS
+PIECE_UNITS = PIECE // BANK
+LEAD = 2
+SHARE = NNEI // UNITS
+TAIL = 3 * BANK
+TAIL_ATOMS = TAIL // NNEI
 
 FLOPS = 2 * C * E * N
 
@@ -30,7 +36,6 @@ def tile_repflowlayer_kernel(tc, x, edge, w_proj, sw, offs, out):
     nc = tc.nc
     x_blocks = x.rearrange("(b p) s -> b p s", p=P)
     out_blocks = out.rearrange("(b p) i -> b p i", p=P)
-    sw_row = sw.rearrange("o n -> (o n)")
 
     with (
         tc.tile_pool(name="held", bufs=1) as held,
@@ -38,81 +43,112 @@ def tile_repflowlayer_kernel(tc, x, edge, w_proj, sw, offs, out):
         tc.tile_pool(name="per_piece", bufs=LEAD + 1) as per_piece,
         tc.tile_pool(name="turned", bufs=2) as turned,
         tc.psum_pool(name="psum_turned", bufs=2) as psum_turned,
-        tc.psum_pool(name="psum_p", bufs=3) as psum_p,
+        tc.psum_pool(name="psum_p", bufs=4) as psum_p,
         tc.psum_pool(name="psum_sums", bufs=2) as psum_sums,
-        tc.psum_pool(name="psum_result", bufs=1) as psum_result,
     ):
         offsets = held.tile([P, N // 16], U16, name="offsets")
         w_sb = held.tile([E, C], BF16, name="w_sb")
         edge_sb = held.tile([E, N], BF16, name="edge_sb")
-        sw_col = held.tile([P, N // P], F32, name="sw_col")
+        sw_rows = held.tile([P, BLOCK], F32, name="sw_rows", align_bytes=64)
+        sw_col = held.tile([P, GROUPS], F32, name="sw_col", align_bytes=64)
         identity = held.tile([P, P], F32, name="identity")
         x_tiles = [held.tile([P, S], F32, name=f"x{b}") for b in range(BLOCKS)]
 
+        last_msg = held.tile([P, N], F32, name="last_msg")
+        tail_msg = held.tile([P, TAIL], F32, name="tail_msg")
+
         make_identity(nc, identity[:])
+        warm_in = held.tile([P, 1], F32, name="warm_in")
+        warm_out = held.tile([P, 1], F32, name="warm_out")
+        nc.vector.memset(warm_in[:], 0.0)
+        nc.scalar.activation(warm_out[:], warm_in[:], COPY)
+        nc.gpsimd.memset(last_msg[:, N - TAIL : N], 0.0)
 
         def in_list(k):
             return slice(k * PIECE, (k + 1) * PIECE)
 
-        def load_switch(k):
-            with nc.allow_non_contiguous_dma(reason="one value of sw to a partition"):
-                nc.sync.dma_start(
-                    sw_col[:, k * (PIECE // P) : (k + 1) * (PIECE // P)],
-                    sw_row[in_list(k)].rearrange("(g p) -> p g", p=P),
-                )
+        def load_edge(k):
+            nc.sync.dma_start(edge_sb[:, in_list(k)], edge[:, in_list(k)])
 
-        load_switch(0)
-        nc.sync.dma_start(offsets[:], offs)
+        nc.scalar.dma_start(w_sb[:, 0:P], w_proj[:, 0:P])
+        load_edge(0)
+        sw_quarters = sw.rearrange("o (g a c) -> (o a) g c", a=QUARTERS, c=BLOCK)
+        for a in range(QUARTERS):
+            nc.sync.dma_start(sw_rows[a * BLOCK : (a + 1) * BLOCK, :], sw_quarters[a])
+        load_edge(1)
         nc.sync.dma_start(x_tiles[0][:], x_blocks[0])
-        for k in range(PIECES):
-            nc.scalar.dma_start(edge_sb[:, in_list(k)], edge[:, in_list(k)])
-            if k == 0:
-                nc.scalar.dma_start(w_sb[:], w_proj)
-            else:
-                load_switch(k)
+        nc.sync.dma_start(offsets[:], offs)
+        load_edge(2)
+        load_edge(3)
+        nc.sync.dma_start(w_sb[:, P:C], w_proj[:, P:C])
         for b in range(1, BLOCKS):
             nc.sync.dma_start(x_tiles[b][:], x_blocks[b])
 
-        turned_tiles, p_tiles, msgs, sums_ps, sums_sb, results_ps = {}, {}, {}, {}, {}, {}
+        nc.vector.transpose(sw_col[:], sw_rows[:])
 
-        def project_turned(b, k):
-            turned_tiles[(b, k)] = turned.tile([P, PIECE], F32, name="turned_sb")
-            for h in range(PIECE // BANK):
-                turned_ps = psum_turned.tile([P, BANK], F32, name="turned_ps")
-                for g in range(GROUPS):
-                    j0 = k * PIECE + h * BANK + g * P
-                    nc.tensor.matmul(
-                        turned_ps[:, g * P : (g + 1) * P],
-                        edge_sb[:, j0 : j0 + P],
-                        w_sb[:, b * P : (b + 1) * P],
-                        start=True,
-                        stop=True,
-                    )
-                for g in range(GROUPS):
-                    j0 = k * PIECE + h * BANK + g * P
-                    nc.scalar.activation(
-                        turned_tiles[(b, k)][:, j0 % PIECE : j0 % PIECE + P],
-                        turned_ps[:, g * P : (g + 1) * P],
-                        COPY,
-                        scale=sw_col[:, j0 // P : j0 // P + 1],
-                    )
+        turned_ps, turned_sb, p_tiles, msgs, sums_ps, sums_sb, results_ps = {}, {}, {}, {}, {}, {}, {}
 
-        def finish_p(b, k):
-            p_tiles[(b, k)] = per_piece.tile([P, PIECE], F32, name="p_sb")
-            for h in range(PIECE // BANK):
-                p_ps = psum_p.tile([P, BANK], F32, name="p_ps")
-                for g in range(GROUPS):
-                    j0 = h * BANK + g * P
-                    nc.tensor.transpose(
-                        p_ps[:, g * P : (g + 1) * P], turned_tiles[(b, k)][:, j0 : j0 + P], identity[:]
-                    )
-                nc.scalar.mul(p_tiles[(b, k)][:, h * BANK : (h + 1) * BANK], p_ps[:], 1.0 / NNEI)
+        def p_part(b, u):
+            k, part = divmod(u, PIECE_UNITS)
+            if part == 0:
+                p_tiles[(b, k)] = per_piece.tile([P, PIECE], F32, name="p_sb")
+            return p_tiles[(b, k)][:, part * BANK : (part + 1) * BANK]
 
-        def look_up(b, k):
+        def on_vector(b, u):
+            return b == 0 and u == 0
+
+        def project_turned(b, u):
+            ps = psum_turned.tile([P, BANK], F32, name="turned_ps")
+            sb = turned.tile([P, BANK], F32, name="turned_sb")
+            turned_sb[(b, u)] = sb
+            for g in range(UNIT_GROUPS):
+                j0 = u * BANK + g * P
+                nc.tensor.matmul(
+                    ps[:, g * P : (g + 1) * P],
+                    edge_sb[:, j0 : j0 + P],
+                    w_sb[:, b * P : (b + 1) * P],
+                    start=True,
+                    stop=True,
+                )
+            for g in range(UNIT_GROUPS):
+                columns = slice(g * P, (g + 1) * P)
+                list_group = u * UNIT_GROUPS + g
+                switch = sw_col[:, list_group : list_group + 1]
+                if on_vector(b, u):
+                    nc.vector.tensor_scalar(sb[:, columns], ps[:, columns], switch, None, MULT)
+                else:
+                    nc.scalar.activation(sb[:, columns], ps[:, columns], COPY, scale=switch)
+
+        def finish_p(b, u):
+            p_ps = psum_p.tile([P, BANK], F32, name="p_ps")
+            for g in range(UNIT_GROUPS):
+                columns = slice(g * P, (g + 1) * P)
+                nc.tensor.transpose(p_ps[:, columns], turned_sb[(b, u)][:, columns], identity[:])
+            if on_vector(b, u):
+                nc.vector.tensor_scalar(p_part(b, u), p_ps[:], 1.0 / NNEI, None, MULT)
+            else:
+                nc.scalar.mul(p_part(b, u), p_ps[:], 1.0 / NNEI)
+
+        def look_up(b, k, first, width):
+            j0 = k * PIECE + first
+            picked = x_tiles[b][:].indirect(offsets[:, j0 // 16 : (j0 + width) // 16])
+            in_tail = j0 - (N - TAIL)
+            if b == BLOCKS - 1 and in_tail >= 0:
+                product = tail_msg[:, in_tail : in_tail + width]
+            else:
+                product = msgs[b][:, j0 : j0 + width]
+            nc.vector.tensor_tensor(product, picked, p_tiles[(b, k)][:, first : first + width], MULT)
+
+        def look_up_piece(b, k):
             if k == 0:
-                msgs[b] = per_block.tile([P, N], F32, name="msg")
-            picked = x_tiles[b][:].indirect(offsets[:, k * (PIECE // 16) : (k + 1) * (PIECE // 16)])
-            nc.vector.tensor_tensor(msgs[b][:, in_list(k)], picked, p_tiles[(b, k)][:], MULT)
+                msgs[b] = last_msg if b == BLOCKS - 1 else per_block.tile([P, N], F32, name="msg")
+            is_start = b == 0 and k < 2
+            holds_tail_start = b == BLOCKS - 1 and k == (N - TAIL) // PIECE
+            if is_start or holds_tail_start:
+                for part in range(PIECE_UNITS):
+                    look_up(b, k, part * BANK, BANK)
+            else:
+                look_up(b, k, 0, PIECE)
 
         def add_up(b, share):
             def add_transposed(columns, start, stop):
@@ -121,49 +157,52 @@ def tile_repflowlayer_kernel(tc, x, edge, w_proj, sw, offs, out):
                 )
 
             if share == 0:
-                sums_ps[b] = psum_sums.tile([NLOC, BANK], F32, name="sums_ps")
-                add_transposed(x_tiles[b][:, 0:NLOC], True, False)
+                sums_ps[b] = psum_sums.tile([NLOC, BANK], F32, name="sums_ps", tag="sums")
             by_atom = msgs[b][:].rearrange("p (i t) -> p i t", t=NNEI)
             for t in range(share * SHARE, (share + 1) * SHARE):
-                add_transposed(by_atom[:, :, t], False, t == NNEI - 1)
+                add_transposed(by_atom[:, :, t], t == 0, False)
+            if share == UNITS - 1:
+                add_transposed(x_tiles[b][:, 0:NLOC], False, True)
 
         def scale(b):
             sums_sb[b] = per_block.tile([NLOC, P], F32, name="sums_sb")
             nc.scalar.mul(sums_sb[b][:], sums_ps[b][:, 0:P], 1.0 / math.sqrt(5.0))
 
         def turn_back(b):
-            results_ps[b] = psum_result.tile([P, BANK], F32, name="result_ps")
+            results_ps[b] = psum_sums.tile([P, BANK], F32, name="result_ps", tag="sums")
             nc.tensor.transpose(results_ps[b][:, 0:NLOC], sums_sb[b][:], identity[:])
 
         def store(b):
+            atoms = NLOC - TAIL_ATOMS if b == BLOCKS - 1 else NLOC
             result = per_block.tile([P, NLOC], F32, name="result")
-            nc.scalar.copy(result[:], results_ps[b][:, 0:NLOC])
-            nc.sync.dma_start(out_blocks[b], result[:])
+            nc.scalar.copy(result[:, 0:atoms], results_ps[b][:, 0:atoms])
+            nc.sync.dma_start(out_blocks[b][:, 0:atoms], result[:, 0:atoms])
 
-        def finish_on_vector(b):
-            own = held.tile([P, NLOC], F32, name="own")
-            nc.scalar.mul(own[:], x_tiles[b][:, 0:NLOC], 1.0 / math.sqrt(5.0))
-            sums = held.tile([P, NLOC], F32, name="sums")
+        def finish_tail():
+            b = BLOCKS - 1
+            own = held.tile([P, TAIL_ATOMS], F32, name="own")
+            nc.scalar.mul(own[:], x_tiles[b][:, NLOC - TAIL_ATOMS : NLOC], 1.0 / math.sqrt(5.0))
+            sums = held.tile([P, TAIL_ATOMS], F32, name="sums")
             nc.vector.tensor_reduce(
-                sums[:], msgs[b][:].rearrange("p (i t) -> p i t", t=NNEI), axis=mybir.AxisListType.X, op=ADD
+                sums[:], tail_msg[:].rearrange("p (i t) -> p i t", t=NNEI), axis=mybir.AxisListType.X, op=ADD
             )
-            result = per_block.tile([P, NLOC], F32, name="result")
+            result = held.tile([P, TAIL_ATOMS], F32, name="tail_result")
             nc.vector.scalar_tensor_tensor(result[:], sums[:], 1.0 / math.sqrt(5.0), own[:], MULT, ADD)
-            nc.sync.dma_start(out_blocks[b], result[:])
+            nc.sync.dma_start(out_blocks[b][:, NLOC - TAIL_ATOMS : NLOC], result[:])
 
-        after = [lambda b, share=share: add_up(b, share) for share in range(PIECES)] + [scale, turn_back, store]
+        after = [lambda b, share=share: add_up(b, share) for share in range(UNITS)] + [scale, turn_back, store]
 
-        for n in range(STEPS + 1 + LEAD + len(after) - PIECES):
+        for n in range(STEPS + 1 + LEAD * PIECE_UNITS + len(after)):
             if n < STEPS:
-                project_turned(n // PIECES, n % PIECES)
+                project_turned(n // UNITS, n % UNITS)
             if 0 <= n - 1 < STEPS:
-                finish_p((n - 1) // PIECES, (n - 1) % PIECES)
-            m = n - 1 - LEAD
-            if 0 <= m < STEPS:
-                look_up(m // PIECES, m % PIECES)
+                finish_p((n - 1) // UNITS, (n - 1) % UNITS)
+            m = n - 1 - LEAD * PIECE_UNITS
+            if 0 <= m < STEPS and m % PIECE_UNITS == PIECE_UNITS - 1:
+                look_up_piece(m // UNITS, m % UNITS // PIECE_UNITS)
             for turn, entry in enumerate(after):
-                b, k = divmod(m - turn, PIECES)
-                if k == PIECES - 1 and 0 <= b < BLOCKS - 1:
+                b, u = divmod(m - turn, UNITS)
+                if u == UNITS - 1 and 0 <= b < BLOCKS:
                     entry(b)
             if m == STEPS - 1:
-                finish_on_vector(BLOCKS - 1)
+                finish_tail()

@@ -1,13 +1,13 @@
 import math
 
 import concourse.mybir as mybir
-from concourse.masks import make_identity
 
 F32 = mybir.dt.float32
 BF16 = mybir.dt.bfloat16
 U16 = mybir.dt.uint16
 MULT = mybir.AluOpType.mult
 ADD = mybir.AluOpType.add
+IS_EQUAL = mybir.AluOpType.is_equal
 COPY = mybir.ActivationFunctionType.Copy
 
 P = 128
@@ -41,9 +41,9 @@ def tile_repflowlayer_kernel(tc, x, edge, w_proj, sw, offs, out):
         tc.tile_pool(name="held", bufs=1) as held,
         tc.tile_pool(name="per_block", bufs=3) as per_block,
         tc.tile_pool(name="per_piece", bufs=LEAD + 1) as per_piece,
-        tc.tile_pool(name="turned", bufs=2) as turned,
-        tc.psum_pool(name="psum_turned", bufs=2) as psum_turned,
-        tc.psum_pool(name="psum_p", bufs=4) as psum_p,
+        tc.tile_pool(name="turned", bufs=3) as turned,
+        tc.psum_pool(name="psum_turned", bufs=3) as psum_turned,
+        tc.psum_pool(name="psum_p", bufs=3) as psum_p,
         tc.psum_pool(name="psum_sums", bufs=2) as psum_sums,
     ):
         offsets = held.tile([P, N // 16], U16, name="offsets")
@@ -57,7 +57,18 @@ def tile_repflowlayer_kernel(tc, x, edge, w_proj, sw, offs, out):
         last_msg = held.tile([P, N], F32, name="last_msg")
         tail_msg = held.tile([P, TAIL], F32, name="tail_msg")
 
-        make_identity(nc, identity[:])
+        ones = held.tile([P, BLOCK], F32, name="ones")
+        along_columns = held.tile([P, BLOCK], F32, name="along_columns", align_bytes=64)
+        along_partitions = held.tile([P, BLOCK], F32, name="along_partitions", align_bytes=64)
+        nc.vector.memset(ones[:], 1.0)
+        nc.vector.memset(identity[:], 0.0)
+        nc.vector.tensor_tensor_scan(along_columns[:], ones[:], ones[:], 0.0, MULT, ADD)
+        nc.vector.transpose(along_partitions[:], along_columns[:])
+        for a in range(QUARTERS):
+            block = slice(a * BLOCK, (a + 1) * BLOCK)
+            nc.vector.tensor_tensor(
+                identity[block, block], along_columns[block, :], along_partitions[block, :], IS_EQUAL
+            )
         warm_in = held.tile([P, 1], F32, name="warm_in")
         warm_out = held.tile([P, 1], F32, name="warm_out")
         nc.vector.memset(warm_in[:], 0.0)
@@ -94,8 +105,7 @@ def tile_repflowlayer_kernel(tc, x, edge, w_proj, sw, offs, out):
                 p_tiles[(b, k)] = per_piece.tile([P, PIECE], F32, name="p_sb")
             return p_tiles[(b, k)][:, part * BANK : (part + 1) * BANK]
 
-        def on_vector(b, u):
-            return b == 0 and u == 0
+        turned_by_vector, finished_by_vector = (0, 1), (0, 0)
 
         def project_turned(b, u):
             ps = psum_turned.tile([P, BANK], F32, name="turned_ps")
@@ -114,7 +124,7 @@ def tile_repflowlayer_kernel(tc, x, edge, w_proj, sw, offs, out):
                 columns = slice(g * P, (g + 1) * P)
                 list_group = u * UNIT_GROUPS + g
                 switch = sw_col[:, list_group : list_group + 1]
-                if on_vector(b, u):
+                if (b, u) == turned_by_vector:
                     nc.vector.tensor_scalar(sb[:, columns], ps[:, columns], switch, None, MULT)
                 else:
                     nc.scalar.activation(sb[:, columns], ps[:, columns], COPY, scale=switch)
@@ -124,7 +134,7 @@ def tile_repflowlayer_kernel(tc, x, edge, w_proj, sw, offs, out):
             for g in range(UNIT_GROUPS):
                 columns = slice(g * P, (g + 1) * P)
                 nc.tensor.transpose(p_ps[:, columns], turned_sb[(b, u)][:, columns], identity[:])
-            if on_vector(b, u):
+            if (b, u) == finished_by_vector:
                 nc.vector.tensor_scalar(p_part(b, u), p_ps[:], 1.0 / NNEI, None, MULT)
             else:
                 nc.scalar.mul(p_part(b, u), p_ps[:], 1.0 / NNEI)
@@ -142,7 +152,7 @@ def tile_repflowlayer_kernel(tc, x, edge, w_proj, sw, offs, out):
         def look_up_piece(b, k):
             if k == 0:
                 msgs[b] = last_msg if b == BLOCKS - 1 else per_block.tile([P, N], F32, name="msg")
-            is_start = b == 0 and k < 2
+            is_start = b == 0
             holds_tail_start = b == BLOCKS - 1 and k == (N - TAIL) // PIECE
             if is_start or holds_tail_start:
                 for part in range(PIECE_UNITS):

@@ -17,16 +17,21 @@ NLOC, NNEI = 128, 32
 BANK = 512
 PIECE = 1024
 BLOCKS = C // P
+PAIR = 2
+PAIR_C = PAIR * P
 GROUPS = N // P
 BLOCK = 32
 QUARTERS = P // BLOCK
 UNIT_GROUPS = BANK // P
+BANK_GROUPS = BANK // PAIR_C
 UNITS = N // BANK
-STEPS = BLOCKS * UNITS
+STEPS = BLOCKS // PAIR * UNITS
 PIECE_UNITS = PIECE // BANK
-LEAD = 2
-SHARE = NNEI // UNITS
-TAIL = 3 * BANK
+AHEAD = 3
+SUMS_LAG = 2
+RUN = 4
+LAST_PAIR = BLOCKS - PAIR
+TAIL = PIECE
 TAIL_ATOMS = TAIL // NNEI
 
 FLOPS = 2 * C * E * N
@@ -39,8 +44,8 @@ def tile_repflowlayer_kernel(tc, x, edge, w_proj, sw, offs, out):
 
     with (
         tc.tile_pool(name="held", bufs=1) as held,
-        tc.tile_pool(name="per_block", bufs=3) as per_block,
-        tc.tile_pool(name="per_piece", bufs=LEAD + 1) as per_piece,
+        tc.tile_pool(name="per_block", bufs=2 * PAIR) as per_block,
+        tc.tile_pool(name="per_piece", bufs=AHEAD * PAIR) as per_piece,
         tc.tile_pool(name="turned", bufs=3) as turned,
         tc.psum_pool(name="psum_turned", bufs=3) as psum_turned,
         tc.psum_pool(name="psum_p", bufs=3) as psum_p,
@@ -54,8 +59,8 @@ def tile_repflowlayer_kernel(tc, x, edge, w_proj, sw, offs, out):
         identity = held.tile([P, P], F32, name="identity")
         x_tiles = [held.tile([P, S], F32, name=f"x{b}") for b in range(BLOCKS)]
 
-        last_msg = held.tile([P, N], F32, name="last_msg")
-        tail_msg = held.tile([P, TAIL], F32, name="tail_msg")
+        last_msgs = [held.tile([P, N], F32, name=f"last_msg{side}") for side in range(PAIR)]
+        tail_msg = held.tile([P, PAIR * TAIL], F32, name="tail_msg")
 
         ones = held.tile([P, BLOCK], F32, name="ones")
         along_columns = held.tile([P, BLOCK], F32, name="along_columns", align_bytes=64)
@@ -73,7 +78,8 @@ def tile_repflowlayer_kernel(tc, x, edge, w_proj, sw, offs, out):
         warm_out = held.tile([P, 1], F32, name="warm_out")
         nc.vector.memset(warm_in[:], 0.0)
         nc.scalar.activation(warm_out[:], warm_in[:], COPY)
-        nc.gpsimd.memset(last_msg[:, N - TAIL : N], 0.0)
+        for last_msg in last_msgs:
+            nc.gpsimd.memset(last_msg[:, N - TAIL : N], 0.0)
 
         def in_list(k):
             return slice(k * PIECE, (k + 1) * PIECE)
@@ -81,7 +87,7 @@ def tile_repflowlayer_kernel(tc, x, edge, w_proj, sw, offs, out):
         def load_edge(k):
             nc.sync.dma_start(edge_sb[:, in_list(k)], edge[:, in_list(k)])
 
-        nc.scalar.dma_start(w_sb[:, 0:P], w_proj[:, 0:P])
+        nc.scalar.dma_start(w_sb[:, 0:PAIR_C], w_proj[:, 0:PAIR_C])
         load_edge(0)
         sw_quarters = sw.rearrange("o (g a c) -> (o a) g c", a=QUARTERS, c=BLOCK)
         for a in range(QUARTERS):
@@ -89,15 +95,16 @@ def tile_repflowlayer_kernel(tc, x, edge, w_proj, sw, offs, out):
         load_edge(1)
         nc.sync.dma_start(x_tiles[0][:], x_blocks[0])
         nc.sync.dma_start(offsets[:], offs)
+        nc.sync.dma_start(x_tiles[1][:], x_blocks[1])
         load_edge(2)
         load_edge(3)
-        nc.sync.dma_start(w_sb[:, P:C], w_proj[:, P:C])
-        for b in range(1, BLOCKS):
+        nc.sync.dma_start(w_sb[:, PAIR_C:C], w_proj[:, PAIR_C:C])
+        for b in range(PAIR, BLOCKS):
             nc.sync.dma_start(x_tiles[b][:], x_blocks[b])
 
         nc.vector.transpose(sw_col[:], sw_rows[:])
 
-        turned_ps, turned_sb, p_tiles, msgs, sums_ps, sums_sb, results_ps = {}, {}, {}, {}, {}, {}, {}
+        turned_sb, p_tiles, msgs, sums_ps, sums_sb, results_ps = {}, {}, {}, {}, {}, {}
 
         def p_part(b, u):
             k, part = divmod(u, PIECE_UNITS)
@@ -105,35 +112,40 @@ def tile_repflowlayer_kernel(tc, x, edge, w_proj, sw, offs, out):
                 p_tiles[(b, k)] = per_piece.tile([P, PIECE], F32, name="p_sb")
             return p_tiles[(b, k)][:, part * BANK : (part + 1) * BANK]
 
-        turned_by_vector, finished_by_vector = (0, 1), (0, 0)
+        turned_by_vector, finished_by_vector = (0, 0, 1), (0, 0)
 
-        def project_turned(b, u):
-            ps = psum_turned.tile([P, BANK], F32, name="turned_ps")
-            sb = turned.tile([P, BANK], F32, name="turned_sb")
-            turned_sb[(b, u)] = sb
-            for g in range(UNIT_GROUPS):
-                j0 = u * BANK + g * P
-                nc.tensor.matmul(
-                    ps[:, g * P : (g + 1) * P],
-                    edge_sb[:, j0 : j0 + P],
-                    w_sb[:, b * P : (b + 1) * P],
-                    start=True,
-                    stop=True,
-                )
-            for g in range(UNIT_GROUPS):
-                columns = slice(g * P, (g + 1) * P)
-                list_group = u * UNIT_GROUPS + g
-                switch = sw_col[:, list_group : list_group + 1]
-                if (b, u) == turned_by_vector:
-                    nc.vector.tensor_scalar(sb[:, columns], ps[:, columns], switch, None, MULT)
-                else:
-                    nc.scalar.activation(sb[:, columns], ps[:, columns], COPY, scale=switch)
+        def project_turned(q, u):
+            sb = turned.tile([P, UNIT_GROUPS * PAIR_C], F32, name="turned_sb")
+            turned_sb[(q, u)] = sb
+            for h in range(UNIT_GROUPS // BANK_GROUPS):
+                ps = psum_turned.tile([P, BANK], F32, name="turned_ps")
+                for g in range(BANK_GROUPS):
+                    list_group = u * UNIT_GROUPS + h * BANK_GROUPS + g
+                    nc.tensor.matmul(
+                        ps[:, g * PAIR_C : (g + 1) * PAIR_C],
+                        edge_sb[:, list_group * P : (list_group + 1) * P],
+                        w_sb[:, q * PAIR_C : (q + 1) * PAIR_C],
+                        start=True,
+                        stop=True,
+                    )
+                for g in range(BANK_GROUPS):
+                    list_group = u * UNIT_GROUPS + h * BANK_GROUPS + g
+                    switch = sw_col[:, list_group : list_group + 1]
+                    from_ps = ps[:, g * PAIR_C : (g + 1) * PAIR_C]
+                    to_sb = sb[:, (h * BANK_GROUPS + g) * PAIR_C : (h * BANK_GROUPS + g + 1) * PAIR_C]
+                    if (q, u, h) == turned_by_vector:
+                        nc.vector.tensor_scalar(to_sb, from_ps, switch, None, MULT)
+                    else:
+                        nc.scalar.activation(to_sb, from_ps, COPY, scale=switch)
 
         def finish_p(b, u):
+            q, side = divmod(b, PAIR)
             p_ps = psum_p.tile([P, BANK], F32, name="p_ps")
             for g in range(UNIT_GROUPS):
-                columns = slice(g * P, (g + 1) * P)
-                nc.tensor.transpose(p_ps[:, columns], turned_sb[(b, u)][:, columns], identity[:])
+                c0 = g * PAIR_C + side * P
+                nc.tensor.transpose(
+                    p_ps[:, g * P : (g + 1) * P], turned_sb[(q, u)][:, c0 : c0 + P], identity[:]
+                )
             if (b, u) == finished_by_vector:
                 nc.vector.tensor_scalar(p_part(b, u), p_ps[:], 1.0 / NNEI, None, MULT)
             else:
@@ -142,36 +154,34 @@ def tile_repflowlayer_kernel(tc, x, edge, w_proj, sw, offs, out):
         def look_up(b, k, first, width):
             j0 = k * PIECE + first
             picked = x_tiles[b][:].indirect(offsets[:, j0 // 16 : (j0 + width) // 16])
-            in_tail = j0 - (N - TAIL)
-            if b == BLOCKS - 1 and in_tail >= 0:
-                product = tail_msg[:, in_tail : in_tail + width]
+            if b >= LAST_PAIR and j0 >= N - TAIL:
+                t0 = (b - LAST_PAIR) * TAIL + j0 - (N - TAIL)
+                product = tail_msg[:, t0 : t0 + width]
             else:
                 product = msgs[b][:, j0 : j0 + width]
             nc.vector.tensor_tensor(product, picked, p_tiles[(b, k)][:, first : first + width], MULT)
 
         def look_up_piece(b, k):
             if k == 0:
-                msgs[b] = last_msg if b == BLOCKS - 1 else per_block.tile([P, N], F32, name="msg")
-            is_start = b == 0
-            holds_tail_start = b == BLOCKS - 1 and k == (N - TAIL) // PIECE
-            if is_start or holds_tail_start:
+                msgs[b] = last_msgs[b - LAST_PAIR] if b >= LAST_PAIR else per_block.tile([P, N], F32, name="msg")
+            if b == 0:
                 for part in range(PIECE_UNITS):
                     look_up(b, k, part * BANK, BANK)
             else:
                 look_up(b, k, 0, PIECE)
 
-        def add_up(b, share):
+        def add_up(b, first):
             def add_transposed(columns, start, stop):
                 nc.tensor.matmul(
                     sums_ps[b][:, 0:P], columns, identity[:], start=start, stop=stop, is_transpose=True
                 )
 
-            if share == 0:
+            if first == 0:
                 sums_ps[b] = psum_sums.tile([NLOC, BANK], F32, name="sums_ps", tag="sums")
             by_atom = msgs[b][:].rearrange("p (i t) -> p i t", t=NNEI)
-            for t in range(share * SHARE, (share + 1) * SHARE):
+            for t in range(first, first + RUN):
                 add_transposed(by_atom[:, :, t], t == 0, False)
-            if share == UNITS - 1:
+            if first + RUN == NNEI:
                 add_transposed(x_tiles[b][:, 0:NLOC], False, True)
 
         def scale(b):
@@ -183,36 +193,50 @@ def tile_repflowlayer_kernel(tc, x, edge, w_proj, sw, offs, out):
             nc.tensor.transpose(results_ps[b][:, 0:NLOC], sums_sb[b][:], identity[:])
 
         def store(b):
-            atoms = NLOC - TAIL_ATOMS if b == BLOCKS - 1 else NLOC
+            atoms = NLOC - TAIL_ATOMS if b >= LAST_PAIR else NLOC
             result = per_block.tile([P, NLOC], F32, name="result")
             nc.scalar.copy(result[:, 0:atoms], results_ps[b][:, 0:atoms])
             nc.sync.dma_start(out_blocks[b][:, 0:atoms], result[:, 0:atoms])
 
         def finish_tail():
-            b = BLOCKS - 1
-            own = held.tile([P, TAIL_ATOMS], F32, name="own")
-            nc.scalar.mul(own[:], x_tiles[b][:, NLOC - TAIL_ATOMS : NLOC], 1.0 / math.sqrt(5.0))
-            sums = held.tile([P, TAIL_ATOMS], F32, name="sums")
+            own = held.tile([P, PAIR * TAIL_ATOMS], F32, name="own")
+            sums = held.tile([P, PAIR * TAIL_ATOMS], F32, name="sums")
+            result = held.tile([P, PAIR * TAIL_ATOMS], F32, name="tail_result")
+            for side in range(PAIR):
+                columns = slice(side * TAIL_ATOMS, (side + 1) * TAIL_ATOMS)
+                nc.scalar.mul(
+                    own[:, columns], x_tiles[LAST_PAIR + side][:, NLOC - TAIL_ATOMS : NLOC], 1.0 / math.sqrt(5.0)
+                )
             nc.vector.tensor_reduce(
                 sums[:], tail_msg[:].rearrange("p (i t) -> p i t", t=NNEI), axis=mybir.AxisListType.X, op=ADD
             )
-            result = held.tile([P, TAIL_ATOMS], F32, name="tail_result")
             nc.vector.scalar_tensor_tensor(result[:], sums[:], 1.0 / math.sqrt(5.0), own[:], MULT, ADD)
-            nc.sync.dma_start(out_blocks[b][:, NLOC - TAIL_ATOMS : NLOC], result[:])
+            for side in range(PAIR):
+                columns = slice(side * TAIL_ATOMS, (side + 1) * TAIL_ATOMS)
+                nc.sync.dma_start(out_blocks[LAST_PAIR + side][:, NLOC - TAIL_ATOMS : NLOC], result[:, columns])
 
-        after = [lambda b, share=share: add_up(b, share) for share in range(UNITS)] + [scale, turn_back, store]
+        runs = NNEI // RUN
+        todo = {}
+        for b in range(BLOCKS):
+            last = (UNITS - 1 - TAIL // BANK) if b >= LAST_PAIR else UNITS - 1
+            turn = b // PAIR * UNITS + last + SUMS_LAG + b % PAIR * (runs // 2)
+            for r in range(runs):
+                todo.setdefault((turn + r // 2, r % 2), []).append(lambda b=b, r=r: add_up(b, r * RUN))
+            for i, entry in enumerate((scale, turn_back, store)):
+                todo.setdefault((turn + runs // 2 + i, 0), []).append(lambda b=b, entry=entry: entry(b))
 
-        for n in range(STEPS + 1 + LEAD * PIECE_UNITS + len(after)):
+        for n in range(STEPS + 1 + SUMS_LAG + 2 * runs):
+            m = n - 1
+            q, u = divmod(m, UNITS)
             if n < STEPS:
                 project_turned(n // UNITS, n % UNITS)
-            if 0 <= n - 1 < STEPS:
-                finish_p((n - 1) // UNITS, (n - 1) % UNITS)
-            m = n - 1 - LEAD * PIECE_UNITS
-            if 0 <= m < STEPS and m % PIECE_UNITS == PIECE_UNITS - 1:
-                look_up_piece(m // UNITS, m % UNITS // PIECE_UNITS)
-            for turn, entry in enumerate(after):
-                b, u = divmod(m - turn, UNITS)
-                if u == UNITS - 1 and 0 <= b < BLOCKS:
-                    entry(b)
+            for side in range(PAIR):
+                if 0 <= m < STEPS:
+                    finish_p(q * PAIR + side, u)
+                for entry in todo.get((m, side), []):
+                    entry()
+            if 0 <= m < STEPS and u % PIECE_UNITS == PIECE_UNITS - 1:
+                for side in range(PAIR):
+                    look_up_piece(q * PAIR + side, u // PIECE_UNITS)
             if m == STEPS - 1:
                 finish_tail()

@@ -17,21 +17,19 @@ NLOC, NNEI = 128, 32
 BANK = 512
 PIECE = 1024
 BLOCKS = C // P
-PAIR = 2
-PAIR_C = PAIR * P
+TEAMS = [range(0, 1), range(1, 3), range(3, 5), range(5, 7), range(7, 8)]
+LARGEST = 2
 GROUPS = N // P
 BLOCK = 32
 QUARTERS = P // BLOCK
 UNIT_GROUPS = BANK // P
-BANK_GROUPS = BANK // PAIR_C
 UNITS = N // BANK
-STEPS = BLOCKS // PAIR * UNITS
 PIECE_UNITS = PIECE // BANK
 AHEAD = 3
-SUMS_LAG = 2
+SUMS_LAG = 4
 RUN = 4
-LAST_PAIR = BLOCKS - PAIR
-TAIL = PIECE
+RUNS = NNEI // RUN
+TAIL = 3 * BANK
 TAIL_ATOMS = TAIL // NNEI
 
 FLOPS = 2 * C * E * N
@@ -44,8 +42,8 @@ def tile_repflowlayer_kernel(tc, x, edge, w_proj, sw, offs, out):
 
     with (
         tc.tile_pool(name="held", bufs=1) as held,
-        tc.tile_pool(name="per_block", bufs=2 * PAIR) as per_block,
-        tc.tile_pool(name="per_piece", bufs=AHEAD * PAIR) as per_piece,
+        tc.tile_pool(name="per_block", bufs=2 * LARGEST) as per_block,
+        tc.tile_pool(name="per_piece", bufs=AHEAD * LARGEST) as per_piece,
         tc.tile_pool(name="turned", bufs=3) as turned,
         tc.psum_pool(name="psum_turned", bufs=3) as psum_turned,
         tc.psum_pool(name="psum_p", bufs=3) as psum_p,
@@ -59,8 +57,8 @@ def tile_repflowlayer_kernel(tc, x, edge, w_proj, sw, offs, out):
         identity = held.tile([P, P], F32, name="identity")
         x_tiles = [held.tile([P, S], F32, name=f"x{b}") for b in range(BLOCKS)]
 
-        last_msgs = [held.tile([P, N], F32, name=f"last_msg{side}") for side in range(PAIR)]
-        tail_msg = held.tile([P, PAIR * TAIL], F32, name="tail_msg")
+        last_msg = held.tile([P, N], F32, name="last_msg")
+        tail_msg = held.tile([P, TAIL], F32, name="tail_msg")
 
         ones = held.tile([P, BLOCK], F32, name="ones")
         along_columns = held.tile([P, BLOCK], F32, name="along_columns", align_bytes=64)
@@ -78,8 +76,7 @@ def tile_repflowlayer_kernel(tc, x, edge, w_proj, sw, offs, out):
         warm_out = held.tile([P, 1], F32, name="warm_out")
         nc.vector.memset(warm_in[:], 0.0)
         nc.scalar.activation(warm_out[:], warm_in[:], COPY)
-        for last_msg in last_msgs:
-            nc.gpsimd.memset(last_msg[:, N - TAIL : N], 0.0)
+        nc.gpsimd.memset(last_msg[:, N - TAIL : N], 0.0)
 
         def in_list(k):
             return slice(k * PIECE, (k + 1) * PIECE)
@@ -87,7 +84,7 @@ def tile_repflowlayer_kernel(tc, x, edge, w_proj, sw, offs, out):
         def load_edge(k):
             nc.sync.dma_start(edge_sb[:, in_list(k)], edge[:, in_list(k)])
 
-        nc.scalar.dma_start(w_sb[:, 0:PAIR_C], w_proj[:, 0:PAIR_C])
+        nc.scalar.dma_start(w_sb[:, 0:P], w_proj[:, 0:P])
         load_edge(0)
         sw_quarters = sw.rearrange("o (g a c) -> (o a) g c", a=QUARTERS, c=BLOCK)
         for a in range(QUARTERS):
@@ -95,16 +92,15 @@ def tile_repflowlayer_kernel(tc, x, edge, w_proj, sw, offs, out):
         load_edge(1)
         nc.sync.dma_start(x_tiles[0][:], x_blocks[0])
         nc.sync.dma_start(offsets[:], offs)
-        nc.sync.dma_start(x_tiles[1][:], x_blocks[1])
         load_edge(2)
         load_edge(3)
-        nc.sync.dma_start(w_sb[:, PAIR_C:C], w_proj[:, PAIR_C:C])
-        for b in range(PAIR, BLOCKS):
+        nc.sync.dma_start(w_sb[:, P:C], w_proj[:, P:C])
+        for b in range(1, BLOCKS):
             nc.sync.dma_start(x_tiles[b][:], x_blocks[b])
 
         nc.vector.transpose(sw_col[:], sw_rows[:])
 
-        turned_sb, p_tiles, msgs, sums_ps, sums_sb, results_ps = {}, {}, {}, {}, {}, {}
+        turned_parts, p_tiles, msgs, sums_ps, sums_sb, results_ps = {}, {}, {}, {}, {}, {}
 
         def p_part(b, u):
             k, part = divmod(u, PIECE_UNITS)
@@ -112,40 +108,32 @@ def tile_repflowlayer_kernel(tc, x, edge, w_proj, sw, offs, out):
                 p_tiles[(b, k)] = per_piece.tile([P, PIECE], F32, name="p_sb")
             return p_tiles[(b, k)][:, part * BANK : (part + 1) * BANK]
 
-        turned_by_vector, finished_by_vector = (0, 0, 1), (0, 0)
+        turned_by_vector, finished_by_vector = (0, 1), (0, 0)
 
-        def project_turned(q, u):
-            sb = turned.tile([P, UNIT_GROUPS * PAIR_C], F32, name="turned_sb")
-            turned_sb[(q, u)] = sb
-            for h in range(UNIT_GROUPS // BANK_GROUPS):
-                ps = psum_turned.tile([P, BANK], F32, name="turned_ps")
-                for g in range(BANK_GROUPS):
-                    list_group = u * UNIT_GROUPS + h * BANK_GROUPS + g
-                    nc.tensor.matmul(
-                        ps[:, g * PAIR_C : (g + 1) * PAIR_C],
-                        edge_sb[:, list_group * P : (list_group + 1) * P],
-                        w_sb[:, q * PAIR_C : (q + 1) * PAIR_C],
-                        start=True,
-                        stop=True,
-                    )
-                for g in range(BANK_GROUPS):
-                    list_group = u * UNIT_GROUPS + h * BANK_GROUPS + g
+        def project_turned(team, u):
+            channels = slice(team[0] * P, (team[-1] + 1) * P)
+            width = len(team) * P
+            sb = turned.tile([P, UNIT_GROUPS, width], F32, name=f"turned{len(team)}_sb")
+            bank_groups = BANK // width
+            for g0 in range(0, UNIT_GROUPS, bank_groups):
+                ps = psum_turned.tile([P, bank_groups, width], F32, name=f"turned{len(team)}_ps", tag="turned_ps")
+                for g in range(bank_groups):
+                    j0 = u * BANK + (g0 + g) * P
+                    nc.tensor.matmul(ps[:, g, :], edge_sb[:, j0 : j0 + P], w_sb[:, channels], start=True, stop=True)
+                for g in range(bank_groups):
+                    list_group = u * UNIT_GROUPS + g0 + g
                     switch = sw_col[:, list_group : list_group + 1]
-                    from_ps = ps[:, g * PAIR_C : (g + 1) * PAIR_C]
-                    to_sb = sb[:, (h * BANK_GROUPS + g) * PAIR_C : (h * BANK_GROUPS + g + 1) * PAIR_C]
-                    if (q, u, h) == turned_by_vector:
-                        nc.vector.tensor_scalar(to_sb, from_ps, switch, None, MULT)
+                    if (team[0], u) == turned_by_vector:
+                        nc.vector.tensor_scalar(sb[:, g0 + g, :], ps[:, g, :], switch, None, MULT)
                     else:
-                        nc.scalar.activation(to_sb, from_ps, COPY, scale=switch)
+                        nc.scalar.activation(sb[:, g0 + g, :], ps[:, g, :], COPY, scale=switch)
+            for side, b in enumerate(team):
+                turned_parts[(b, u)] = sb[:, :, side * P : (side + 1) * P]
 
         def finish_p(b, u):
-            q, side = divmod(b, PAIR)
             p_ps = psum_p.tile([P, BANK], F32, name="p_ps")
             for g in range(UNIT_GROUPS):
-                c0 = g * PAIR_C + side * P
-                nc.tensor.transpose(
-                    p_ps[:, g * P : (g + 1) * P], turned_sb[(q, u)][:, c0 : c0 + P], identity[:]
-                )
+                nc.tensor.transpose(p_ps[:, g * P : (g + 1) * P], turned_parts[(b, u)][:, g, :], identity[:])
             if (b, u) == finished_by_vector:
                 nc.vector.tensor_scalar(p_part(b, u), p_ps[:], 1.0 / NNEI, None, MULT)
             else:
@@ -154,17 +142,18 @@ def tile_repflowlayer_kernel(tc, x, edge, w_proj, sw, offs, out):
         def look_up(b, k, first, width):
             j0 = k * PIECE + first
             picked = x_tiles[b][:].indirect(offsets[:, j0 // 16 : (j0 + width) // 16])
-            if b >= LAST_PAIR and j0 >= N - TAIL:
-                t0 = (b - LAST_PAIR) * TAIL + j0 - (N - TAIL)
-                product = tail_msg[:, t0 : t0 + width]
+            in_tail = j0 - (N - TAIL)
+            if b == BLOCKS - 1 and in_tail >= 0:
+                product = tail_msg[:, in_tail : in_tail + width]
             else:
                 product = msgs[b][:, j0 : j0 + width]
             nc.vector.tensor_tensor(product, picked, p_tiles[(b, k)][:, first : first + width], MULT)
 
         def look_up_piece(b, k):
             if k == 0:
-                msgs[b] = last_msgs[b - LAST_PAIR] if b >= LAST_PAIR else per_block.tile([P, N], F32, name="msg")
-            if b == 0:
+                msgs[b] = last_msg if b == BLOCKS - 1 else per_block.tile([P, N], F32, name="msg")
+            holds_tail_start = b == BLOCKS - 1 and k == (N - TAIL) // PIECE
+            if b == 0 or holds_tail_start:
                 for part in range(PIECE_UNITS):
                     look_up(b, k, part * BANK, BANK)
             else:
@@ -193,50 +182,53 @@ def tile_repflowlayer_kernel(tc, x, edge, w_proj, sw, offs, out):
             nc.tensor.transpose(results_ps[b][:, 0:NLOC], sums_sb[b][:], identity[:])
 
         def store(b):
-            atoms = NLOC - TAIL_ATOMS if b >= LAST_PAIR else NLOC
+            atoms = NLOC - TAIL_ATOMS if b == BLOCKS - 1 else NLOC
             result = per_block.tile([P, NLOC], F32, name="result")
             nc.scalar.copy(result[:, 0:atoms], results_ps[b][:, 0:atoms])
             nc.sync.dma_start(out_blocks[b][:, 0:atoms], result[:, 0:atoms])
 
         def finish_tail():
-            own = held.tile([P, PAIR * TAIL_ATOMS], F32, name="own")
-            sums = held.tile([P, PAIR * TAIL_ATOMS], F32, name="sums")
-            result = held.tile([P, PAIR * TAIL_ATOMS], F32, name="tail_result")
-            for side in range(PAIR):
-                columns = slice(side * TAIL_ATOMS, (side + 1) * TAIL_ATOMS)
-                nc.scalar.mul(
-                    own[:, columns], x_tiles[LAST_PAIR + side][:, NLOC - TAIL_ATOMS : NLOC], 1.0 / math.sqrt(5.0)
-                )
+            b = BLOCKS - 1
+            own = held.tile([P, TAIL_ATOMS], F32, name="own")
+            nc.scalar.mul(own[:], x_tiles[b][:, NLOC - TAIL_ATOMS : NLOC], 1.0 / math.sqrt(5.0))
+            sums = held.tile([P, TAIL_ATOMS], F32, name="sums")
             nc.vector.tensor_reduce(
                 sums[:], tail_msg[:].rearrange("p (i t) -> p i t", t=NNEI), axis=mybir.AxisListType.X, op=ADD
             )
+            result = held.tile([P, TAIL_ATOMS], F32, name="tail_result")
             nc.vector.scalar_tensor_tensor(result[:], sums[:], 1.0 / math.sqrt(5.0), own[:], MULT, ADD)
-            for side in range(PAIR):
-                columns = slice(side * TAIL_ATOMS, (side + 1) * TAIL_ATOMS)
-                nc.sync.dma_start(out_blocks[LAST_PAIR + side][:, NLOC - TAIL_ATOMS : NLOC], result[:, columns])
+            nc.sync.dma_start(out_blocks[b][:, NLOC - TAIL_ATOMS : NLOC], result[:])
 
-        runs = NNEI // RUN
         todo = {}
-        for b in range(BLOCKS):
-            last = (UNITS - 1 - TAIL // BANK) if b >= LAST_PAIR else UNITS - 1
-            turn = b // PAIR * UNITS + last + SUMS_LAG + b % PAIR * (runs // 2)
-            for r in range(runs):
-                todo.setdefault((turn + r // 2, r % 2), []).append(lambda b=b, r=r: add_up(b, r * RUN))
-            for i, entry in enumerate((scale, turn_back, store)):
-                todo.setdefault((turn + runs // 2 + i, 0), []).append(lambda b=b, entry=entry: entry(b))
+        start = 0
+        for team in TEAMS:
+            for b in team:
+                start = max(start, (team[-1] + 1) * UNITS + SUMS_LAG)
+                for r in range(RUNS):
+                    todo.setdefault(start + r, []).append(lambda b=b, r=r: add_up(b, r * RUN))
+                start += RUNS
+                for i, entry in enumerate((scale, turn_back, store)):
+                    todo.setdefault(start + i, []).append(lambda b=b, entry=entry: entry(b))
+        last_entry = max(todo)
 
-        for n in range(STEPS + 1 + SUMS_LAG + 2 * runs):
-            m = n - 1
-            q, u = divmod(m, UNITS)
-            if n < STEPS:
-                project_turned(n // UNITS, n % UNITS)
-            for side in range(PAIR):
-                if 0 <= m < STEPS:
-                    finish_p(q * PAIR + side, u)
-                for entry in todo.get((m, side), []):
-                    entry()
-            if 0 <= m < STEPS and u % PIECE_UNITS == PIECE_UNITS - 1:
-                for side in range(PAIR):
-                    look_up_piece(q * PAIR + side, u // PIECE_UNITS)
-            if m == STEPS - 1:
-                finish_tail()
+        def do_what_follows(made):
+            for entry in todo.get(made, []):
+                entry()
+
+        turns = [(team, u) for team in TEAMS for u in range(UNITS)]
+        made = 0
+        for n in range(len(turns) + 1):
+            if n < len(turns):
+                project_turned(*turns[n])
+            if n > 0:
+                team, u = turns[n - 1]
+                for b in team:
+                    finish_p(b, u)
+                    made += 1
+                    do_what_follows(made)
+                if u % PIECE_UNITS == PIECE_UNITS - 1:
+                    for b in team:
+                        look_up_piece(b, u // PIECE_UNITS)
+        finish_tail()
+        for made in range(BLOCKS * UNITS + 1, last_entry + 1):
+            do_what_follows(made)

@@ -17,7 +17,7 @@ NLOC, NNEI = 128, 32
 BANK = 512
 PIECE = 1024
 BLOCKS = C // P
-TEAMS = [range(0, 1), range(1, 3), range(3, 5), range(5, 7), range(7, 8)]
+TEAMS = [range(0, 2), range(2, 4), range(4, 6), range(6, 7), range(7, 8)]
 LARGEST = 2
 GROUPS = N // P
 BLOCK = 32
@@ -27,10 +27,9 @@ UNITS = N // BANK
 PIECE_UNITS = PIECE // BANK
 AHEAD = 3
 SUMS_LAG = 4
-RUN = 4
-RUNS = NNEI // RUN
-TAIL = 3 * BANK
+TAIL = PIECE
 TAIL_ATOMS = TAIL // NNEI
+HALF = NNEI // 2
 
 FLOPS = 2 * C * E * N
 
@@ -59,6 +58,7 @@ def tile_repflowlayer_kernel(tc, x, edge, w_proj, sw, offs, out):
 
         last_msg = held.tile([P, N], F32, name="last_msg")
         tail_msg = held.tile([P, TAIL], F32, name="tail_msg")
+        half_sums = held.tile([P, NLOC], F32, name="half_sums")
 
         ones = held.tile([P, BLOCK], F32, name="ones")
         along_columns = held.tile([P, BLOCK], F32, name="along_columns", align_bytes=64)
@@ -77,6 +77,7 @@ def tile_repflowlayer_kernel(tc, x, edge, w_proj, sw, offs, out):
         nc.vector.memset(warm_in[:], 0.0)
         nc.scalar.activation(warm_out[:], warm_in[:], COPY)
         nc.gpsimd.memset(last_msg[:, N - TAIL : N], 0.0)
+        nc.vector.memset(half_sums[:], 0.0)
 
         def in_list(k):
             return slice(k * PIECE, (k + 1) * PIECE)
@@ -84,7 +85,8 @@ def tile_repflowlayer_kernel(tc, x, edge, w_proj, sw, offs, out):
         def load_edge(k):
             nc.sync.dma_start(edge_sb[:, in_list(k)], edge[:, in_list(k)])
 
-        nc.scalar.dma_start(w_sb[:, 0:P], w_proj[:, 0:P])
+        first_channels, other_channels = slice(0, len(TEAMS[0]) * P), slice(len(TEAMS[0]) * P, C)
+        nc.scalar.dma_start(w_sb[:, first_channels], w_proj[:, first_channels])
         load_edge(0)
         sw_quarters = sw.rearrange("o (g a c) -> (o a) g c", a=QUARTERS, c=BLOCK)
         for a in range(QUARTERS):
@@ -92,10 +94,11 @@ def tile_repflowlayer_kernel(tc, x, edge, w_proj, sw, offs, out):
         load_edge(1)
         nc.sync.dma_start(x_tiles[0][:], x_blocks[0])
         nc.sync.dma_start(offsets[:], offs)
+        nc.sync.dma_start(x_tiles[1][:], x_blocks[1])
         load_edge(2)
         load_edge(3)
-        nc.sync.dma_start(w_sb[:, P:C], w_proj[:, P:C])
-        for b in range(1, BLOCKS):
+        nc.sync.dma_start(w_sb[:, other_channels], w_proj[:, other_channels])
+        for b in range(2, BLOCKS):
             nc.sync.dma_start(x_tiles[b][:], x_blocks[b])
 
         nc.vector.transpose(sw_col[:], sw_rows[:])
@@ -152,26 +155,30 @@ def tile_repflowlayer_kernel(tc, x, edge, w_proj, sw, offs, out):
         def look_up_piece(b, k):
             if k == 0:
                 msgs[b] = last_msg if b == BLOCKS - 1 else per_block.tile([P, N], F32, name="msg")
-            holds_tail_start = b == BLOCKS - 1 and k == (N - TAIL) // PIECE
-            if b == 0 or holds_tail_start:
+            if b == 0:
                 for part in range(PIECE_UNITS):
                     look_up(b, k, part * BANK, BANK)
             else:
                 look_up(b, k, 0, PIECE)
 
-        def add_up(b, first):
-            def add_transposed(columns, start, stop):
-                nc.tensor.matmul(
-                    sums_ps[b][:, 0:P], columns, identity[:], start=start, stop=stop, is_transpose=True
-                )
+        def terms(b):
+            return NNEI + 1 if b < BLOCKS - 1 else HALF + 2
 
+        def add_up(b, first, end):
             if first == 0:
                 sums_ps[b] = psum_sums.tile([NLOC, BANK], F32, name="sums_ps", tag="sums")
             by_atom = msgs[b][:].rearrange("p (i t) -> p i t", t=NNEI)
-            for t in range(first, first + RUN):
-                add_transposed(by_atom[:, :, t], t == 0, False)
-            if first + RUN == NNEI:
-                add_transposed(x_tiles[b][:, 0:NLOC], False, True)
+            neighbours = NNEI if b < BLOCKS - 1 else HALF
+            for t in range(first, end):
+                if t < neighbours:
+                    columns = by_atom[:, :, t]
+                elif t == neighbours:
+                    columns = x_tiles[b][:, 0:NLOC]
+                else:
+                    columns = half_sums[:]
+                nc.tensor.matmul(
+                    sums_ps[b][:, 0:P], columns, identity[:], start=t == 0, stop=t == terms(b) - 1, is_transpose=True
+                )
 
         def scale(b):
             sums_sb[b] = per_block.tile([NLOC, P], F32, name="sums_sb")
@@ -186,6 +193,12 @@ def tile_repflowlayer_kernel(tc, x, edge, w_proj, sw, offs, out):
             result = per_block.tile([P, NLOC], F32, name="result")
             nc.scalar.copy(result[:, 0:atoms], results_ps[b][:, 0:atoms])
             nc.sync.dma_start(out_blocks[b][:, 0:atoms], result[:, 0:atoms])
+
+        def sum_second_half():
+            by_atom = last_msg[:, 0 : N - TAIL].rearrange("p (i t) -> p i t", t=NNEI)
+            nc.vector.tensor_reduce(
+                half_sums[:, 0 : NLOC - TAIL_ATOMS], by_atom[:, :, HALF:NNEI], axis=mybir.AxisListType.X, op=ADD
+            )
 
         def finish_tail():
             b = BLOCKS - 1
@@ -204,9 +217,11 @@ def tile_repflowlayer_kernel(tc, x, edge, w_proj, sw, offs, out):
         for team in TEAMS:
             for b in team:
                 start = max(start, (team[-1] + 1) * UNITS + SUMS_LAG)
-                for r in range(RUNS):
-                    todo.setdefault(start + r, []).append(lambda b=b, r=r: add_up(b, r * RUN))
-                start += RUNS
+                runs = 8 if b < BLOCKS // 2 else 6
+                cuts = [r * terms(b) // runs for r in range(runs + 1)]
+                for first, end in zip(cuts, cuts[1:]):
+                    todo.setdefault(start, []).append(lambda b=b, first=first, end=end: add_up(b, first, end))
+                    start += 1
                 for i, entry in enumerate((scale, turn_back, store)):
                     todo.setdefault(start + i, []).append(lambda b=b, entry=entry: entry(b))
         last_entry = max(todo)
@@ -215,7 +230,8 @@ def tile_repflowlayer_kernel(tc, x, edge, w_proj, sw, offs, out):
             for entry in todo.get(made, []):
                 entry()
 
-        turns = [(team, u) for team in TEAMS for u in range(UNITS)]
+        turns = [((b,), u) for b in TEAMS[0] for u in range(PIECE_UNITS)]
+        turns += [(team, u) for team in TEAMS for u in range(UNITS)][PIECE_UNITS:]
         made = 0
         for n in range(len(turns) + 1):
             if n < len(turns):
@@ -229,6 +245,7 @@ def tile_repflowlayer_kernel(tc, x, edge, w_proj, sw, offs, out):
                 if u % PIECE_UNITS == PIECE_UNITS - 1:
                     for b in team:
                         look_up_piece(b, u // PIECE_UNITS)
+        sum_second_half()
         finish_tail()
         for made in range(BLOCKS * UNITS + 1, last_entry + 1):
             do_what_follows(made)

import math

import concourse.mybir as mybir

F32 = mybir.dt.float32
BF16 = mybir.dt.bfloat16
U16 = mybir.dt.uint16
MULT = mybir.AluOpType.mult
ADD = mybir.AluOpType.add
IS_EQUAL = mybir.AluOpType.is_equal
COPY = mybir.ActivationFunctionType.Copy

P = 128
C, S = 1024, 2048
E, N = 128, 4096
NLOC, NNEI = 128, 32
BANK = 512
PIECE = 1024
BLOCKS = C // P
TEAMS = [range(0, 2), range(2, 4), range(4, 6), range(6, 7), range(7, 8)]
LARGEST = 2
GROUPS = N // P
BLOCK = 32
QUARTERS = P // BLOCK
UNIT_GROUPS = BANK // P
UNITS = N // BANK
PIECE_UNITS = PIECE // BANK
AHEAD = 3
SUMS_LAG = 4
TAIL = PIECE
TAIL_ATOMS = TAIL // NNEI
HALF = NNEI // 2

FLOPS = 2 * C * E * N


def tile_repflowlayer_kernel(tc, x, edge, w_proj, sw, offs, out):
    nc = tc.nc
    x_blocks = x.rearrange("(b p) s -> b p s", p=P)
    out_blocks = out.rearrange("(b p) i -> b p i", p=P)

    with (
        tc.tile_pool(name="held", bufs=1) as held,
        tc.tile_pool(name="per_block", bufs=2 * LARGEST) as per_block,
        tc.tile_pool(name="per_piece", bufs=AHEAD * LARGEST) as per_piece,
        tc.tile_pool(name="turned", bufs=3) as turned,
        tc.psum_pool(name="psum_turned", bufs=3) as psum_turned,
        tc.psum_pool(name="psum_p", bufs=3) as psum_p,
        tc.psum_pool(name="psum_sums", bufs=2) as psum_sums,
    ):
        offsets = held.tile([P, N // 16], U16, name="offsets")
        w_sb = held.tile([E, C], BF16, name="w_sb")
        edge_sb = held.tile([E, N], BF16, name="edge_sb")
        sw_rows = held.tile([P, BLOCK], F32, name="sw_rows", align_bytes=64)
        sw_col = held.tile([P, GROUPS], F32, name="sw_col", align_bytes=64)
        identity = held.tile([P, P], F32, name="identity")
        x_tiles = [held.tile([P, S], F32, name=f"x{b}") for b in range(BLOCKS)]

        last_msg = held.tile([P, N], F32, name="last_msg")
        tail_msg = held.tile([P, TAIL], F32, name="tail_msg")
        half_sums = held.tile([P, NLOC], F32, name="half_sums")

        ones = held.tile([P, BLOCK], F32, name="ones")
        along_columns = held.tile([P, BLOCK], F32, name="along_columns", align_bytes=64)
        along_partitions = held.tile([P, BLOCK], F32, name="along_partitions", align_bytes=64)
        nc.vector.memset(ones[:], 1.0)
        nc.vector.memset(identity[:], 0.0)
        nc.vector.tensor_tensor_scan(along_columns[:], ones[:], ones[:], 0.0, MULT, ADD)
        nc.vector.transpose(along_partitions[:], along_columns[:])
        for a in range(QUARTERS):
            block = slice(a * BLOCK, (a + 1) * BLOCK)
            nc.vector.tensor_tensor(
                identity[block, block], along_columns[block, :], along_partitions[block, :], IS_EQUAL
            )
        warm_in = held.tile([P, 1], F32, name="warm_in")
        warm_out = held.tile([P, 1], F32, name="warm_out")
        nc.vector.memset(warm_in[:], 0.0)
        nc.scalar.activation(warm_out[:], warm_in[:], COPY)
        nc.gpsimd.memset(last_msg[:, N - TAIL : N], 0.0)
        nc.vector.memset(half_sums[:], 0.0)

        def in_list(k):
            return slice(k * PIECE, (k + 1) * PIECE)

        def load_edge(k):
            nc.sync.dma_start(edge_sb[:, in_list(k)], edge[:, in_list(k)])

        first_channels, other_channels = slice(0, len(TEAMS[0]) * P), slice(len(TEAMS[0]) * P, C)
        nc.scalar.dma_start(w_sb[:, first_channels], w_proj[:, first_channels])
        load_edge(0)
        sw_quarters = sw.rearrange("o (g a c) -> (o a) g c", a=QUARTERS, c=BLOCK)
        for a in range(QUARTERS):
            nc.sync.dma_start(sw_rows[a * BLOCK : (a + 1) * BLOCK, :], sw_quarters[a])
        load_edge(1)
        nc.sync.dma_start(x_tiles[0][:], x_blocks[0])
        nc.sync.dma_start(offsets[:], offs)
        nc.sync.dma_start(x_tiles[1][:], x_blocks[1])
        load_edge(2)
        load_edge(3)
        nc.sync.dma_start(w_sb[:, other_channels], w_proj[:, other_channels])
        for b in range(2, BLOCKS):
            nc.sync.dma_start(x_tiles[b][:], x_blocks[b])

        nc.vector.transpose(sw_col[:], sw_rows[:])

        turned_parts, p_tiles, msgs, sums_ps, sums_sb, results_ps = {}, {}, {}, {}, {}, {}

        def p_part(b, u):
            k, part = divmod(u, PIECE_UNITS)
            if part == 0:
                p_tiles[(b, k)] = per_piece.tile([P, PIECE], F32, name="p_sb")
            return p_tiles[(b, k)][:, part * BANK : (part + 1) * BANK]

        turned_by_vector, finished_by_vector = (0, 1), (0, 0)

        def project_turned(team, u):
            channels = slice(team[0] * P, (team[-1] + 1) * P)
            width = len(team) * P
            sb = turned.tile([P, UNIT_GROUPS, width], F32, name=f"turned{len(team)}_sb")
            bank_groups = BANK // width
            for g0 in range(0, UNIT_GROUPS, bank_groups):
                ps = psum_turned.tile([P, bank_groups, width], F32, name=f"turned{len(team)}_ps", tag="turned_ps")
                for g in range(bank_groups):
                    j0 = u * BANK + (g0 + g) * P
                    nc.tensor.matmul(ps[:, g, :], edge_sb[:, j0 : j0 + P], w_sb[:, channels], start=True, stop=True)
                for g in range(bank_groups):
                    list_group = u * UNIT_GROUPS + g0 + g
                    switch = sw_col[:, list_group : list_group + 1]
                    if (team[0], u) == turned_by_vector:
                        nc.vector.tensor_scalar(sb[:, g0 + g, :], ps[:, g, :], switch, None, MULT)
                    else:
                        nc.scalar.activation(sb[:, g0 + g, :], ps[:, g, :], COPY, scale=switch)
            for side, b in enumerate(team):
                turned_parts[(b, u)] = sb[:, :, side * P : (side + 1) * P]

        def finish_p(b, u):
            p_ps = psum_p.tile([P, BANK], F32, name="p_ps")
            for g in range(UNIT_GROUPS):
                nc.tensor.transpose(p_ps[:, g * P : (g + 1) * P], turned_parts[(b, u)][:, g, :], identity[:])
            if (b, u) == finished_by_vector:
                nc.vector.tensor_scalar(p_part(b, u), p_ps[:], 1.0 / NNEI, None, MULT)
            else:
                nc.scalar.mul(p_part(b, u), p_ps[:], 1.0 / NNEI)

        def look_up(b, k, first, width):
            j0 = k * PIECE + first
            picked = x_tiles[b][:].indirect(offsets[:, j0 // 16 : (j0 + width) // 16])
            in_tail = j0 - (N - TAIL)
            if b == BLOCKS - 1 and in_tail >= 0:
                product = tail_msg[:, in_tail : in_tail + width]
            else:
                product = msgs[b][:, j0 : j0 + width]
            nc.vector.tensor_tensor(product, picked, p_tiles[(b, k)][:, first : first + width], MULT)

        def look_up_piece(b, k):
            if k == 0:
                msgs[b] = last_msg if b == BLOCKS - 1 else per_block.tile([P, N], F32, name="msg")
            if b == 0:
                for part in range(PIECE_UNITS):
                    look_up(b, k, part * BANK, BANK)
            else:
                look_up(b, k, 0, PIECE)

        def terms(b):
            return NNEI + 1 if b < BLOCKS - 1 else HALF + 2

        def add_up(b, first, end):
            if first == 0:
                sums_ps[b] = psum_sums.tile([NLOC, BANK], F32, name="sums_ps", tag="sums")
            by_atom = msgs[b][:].rearrange("p (i t) -> p i t", t=NNEI)
            neighbours = NNEI if b < BLOCKS - 1 else HALF
            for t in range(first, end):
                if t < neighbours:
                    columns = by_atom[:, :, t]
                elif t == neighbours:
                    columns = x_tiles[b][:, 0:NLOC]
                else:
                    columns = half_sums[:]
                nc.tensor.matmul(
                    sums_ps[b][:, 0:P], columns, identity[:], start=t == 0, stop=t == terms(b) - 1, is_transpose=True
                )

        def scale(b):
            sums_sb[b] = per_block.tile([NLOC, P], F32, name="sums_sb")
            nc.scalar.mul(sums_sb[b][:], sums_ps[b][:, 0:P], 1.0 / math.sqrt(5.0))

        def turn_back(b):
            results_ps[b] = psum_sums.tile([P, BANK], F32, name="result_ps", tag="sums")
            nc.tensor.transpose(results_ps[b][:, 0:NLOC], sums_sb[b][:], identity[:])

        def store(b):
            atoms = NLOC - TAIL_ATOMS if b == BLOCKS - 1 else NLOC
            result = per_block.tile([P, NLOC], F32, name="result")
            nc.scalar.copy(result[:, 0:atoms], results_ps[b][:, 0:atoms])
            nc.sync.dma_start(out_blocks[b][:, 0:atoms], result[:, 0:atoms])

        def sum_second_half():
            by_atom = last_msg[:, 0 : N - TAIL].rearrange("p (i t) -> p i t", t=NNEI)
            nc.vector.tensor_reduce(
                half_sums[:, 0 : NLOC - TAIL_ATOMS], by_atom[:, :, HALF:NNEI], axis=mybir.AxisListType.X, op=ADD
            )

        def finish_tail():
            b = BLOCKS - 1
            own = held.tile([P, TAIL_ATOMS], F32, name="own")
            nc.scalar.mul(own[:], x_tiles[b][:, NLOC - TAIL_ATOMS : NLOC], 1.0 / math.sqrt(5.0))
            sums = held.tile([P, TAIL_ATOMS], F32, name="sums")
            nc.vector.tensor_reduce(
                sums[:], tail_msg[:].rearrange("p (i t) -> p i t", t=NNEI), axis=mybir.AxisListType.X, op=ADD
            )
            result = held.tile([P, TAIL_ATOMS], F32, name="tail_result")
            nc.vector.scalar_tensor_tensor(result[:], sums[:], 1.0 / math.sqrt(5.0), own[:], MULT, ADD)
            nc.sync.dma_start(out_blocks[b][:, NLOC - TAIL_ATOMS : NLOC], result[:])

        todo = {}
        start = 0
        for team in TEAMS:
            for b in team:
                start = max(start, (team[-1] + 1) * UNITS + SUMS_LAG)
                runs = 8 if b < BLOCKS // 2 else 6
                cuts = [r * terms(b) // runs for r in range(runs + 1)]
                for first, end in zip(cuts, cuts[1:]):
                    todo.setdefault(start, []).append(lambda b=b, first=first, end=end: add_up(b, first, end))
                    start += 1
                for i, entry in enumerate((scale, turn_back, store)):
                    todo.setdefault(start + i, []).append(lambda b=b, entry=entry: entry(b))
        last_entry = max(todo)

        def do_what_follows(made):
            for entry in todo.get(made, []):
                entry()

        turns = [((b,), u) for b in TEAMS[0] for u in range(PIECE_UNITS)]
        turns += [(team, u) for team in TEAMS for u in range(UNITS)][PIECE_UNITS:]
        made = 0
        for n in range(len(turns) + 1):
            if n < len(turns):
                project_turned(*turns[n])
            if n > 0:
                team, u = turns[n - 1]
                for b in team:
                    finish_p(b, u)
                    made += 1
                    do_what_follows(made)
                if u % PIECE_UNITS == PIECE_UNITS - 1:
                    for b in team:
                        look_up_piece(b, u // PIECE_UNITS)
        sum_second_half()
        finish_tail()
        for made in range(BLOCKS * UNITS + 1, last_entry + 1):
            do_what_follows(made)
